import numpy as np
import ml_dtypes


def mxq(x, axis, fmt="e4m3"):
    dtype, down = {"e4m3": (ml_dtypes.float8_e4m3fn, 7), "e5m2": (ml_dtypes.float8_e5m2, 14)}[fmt]
    v = np.moveaxis(np.asarray(x, np.float32).astype(ml_dtypes.bfloat16).astype(np.float64), axis, -1)
    blocks = v.reshape(v.shape[:-1] + (-1, 32))
    amax = np.abs(blocks).max(-1, keepdims=True)
    byte = np.maximum(np.where(amax > 0, np.frexp(amax)[1] - 1 + 127, 0) - down, 1)
    scale = np.exp2(byte - 127.0)
    codes = (blocks / scale).astype(np.float32).astype(dtype).astype(np.float64)
    return np.moveaxis((codes * scale).reshape(v.shape), -1, axis)


WIDE = False


def mx_kscale(k):
    if not WIDE:
        return np.ones(k)
    levels = np.array([10, -10, 5, -5, 0])
    a = np.random.permutation(np.resize(levels, k // 512 * 4)).reshape(k // 512, 4)
    idx = np.arange(k)
    return np.exp2(a[idx // 512, idx % 128 // 32])


BF16 = ml_dtypes.bfloat16


def bf(x):
    return np.asarray(x, np.float32).astype(BF16)


def f64(x):
    return np.asarray(x).astype(np.float64)


BH, S, D = 2, 1024, 128
ALPHA = 0.99
EPS = 1e-10
LOG_DECAY = np.log(ALPHA ** np.arange(S - 1.0, -1.0, -1.0) + EPS)


def setup_inputs():
    s = mx_kscale(S)
    decay = np.exp(LOG_DECAY)
    c = (decay * s).sum() / decay.sum()
    a = 1.2 / D ** 0.25
    return {"q": bf(np.random.standard_normal((BH, S, D)) * a),
            "k": bf(np.random.standard_normal((BH, S, D)) * a),
            "v": bf(np.random.standard_normal((BH, S, D)) * 2.0 * c / s[:, None]),
            "attn_mask": bf(np.random.standard_normal((BH, S, S)) * 0.5 + np.log(s))}


def reference(q, k, v, attn_mask):
    scores = f64(q) @ f64(k).transpose(0, 2, 1) + f64(attn_mask)
    scores = scores + LOG_DECAY[None, None, :]
    e = np.exp(scores - scores.max(-1, keepdims=True))
    return (mxq(e, 2, "e4m3") @ mxq(f64(v), 1, "e4m3")) / e.sum(-1, keepdims=True)

@@ -1,0 +1,188 @@
+import math
+from contextlib import ExitStack
+
+import concourse.mybir as mybir
+from concourse.masks import make_identity
+
+F32 = mybir.dt.float32
+BF16 = mybir.dt.bfloat16
+I32 = mybir.dt.int32
+U32 = mybir.dt.uint32
+U8 = mybir.dt.uint8
+FP8X4 = mybir.dt.float8_e4m3fn_x4
+ALU = mybir.AluOpType
+ACT = mybir.ActivationFunctionType
+AX = mybir.AxisListType
+
+P = 128
+BH, S, D = 2, 1024, 128
+NT = S // P
+PACK = 4
+KPASS = P * PACK
+NPASS = S // KPASS
+NBLK = NPASS * PACK
+
+ALPHA = 0.99
+EPS = 1e-10
+LN_A = math.log(ALPHA)
+C_HI = round(LN_A * 2.0 ** 20) / 2.0 ** 20
+C_LO = LN_A - C_HI
+
+FLOPS = 2 * 2 * BH * S * S * D
+
+
+def tile_dotproductattention_kernel(tc, q, k, v, attn_mask, out):
+    nc = tc.nc
+    with ExitStack() as ctx:
+        const = ctx.enter_context(tc.tile_pool(name="const", bufs=1))
+        work = ctx.enter_context(tc.tile_pool(name="work", bufs=3))
+        small = ctx.enter_context(tc.tile_pool(name="small", bufs=4))
+        ps_s = ctx.enter_context(tc.psum_pool(name="ps_s", bufs=4))
+        ps_t = ctx.enter_context(tc.psum_pool(name="ps_t", bufs=2))
+        ps_o = ctx.enter_context(tc.psum_pool(name="ps_o", bufs=2))
+
+        k_sb = [const.tile([P, NPASS, PACK, D], BF16, name="k_sb%d" % b) for b in range(BH)]
+        q_sb = [const.tile([P, NT, D], BF16, name="q_sb%d" % b) for b in range(BH)]
+        m_sb = [const.tile([P, NT, S], BF16, name="m_sb%d" % b) for b in range(BH)]
+        v_sb = const.tile([P, BH * NPASS, PACK, D], BF16, name="v_sb")
+        m_dram = [attn_mask[b].rearrange("(p n) j -> p n j", n=NT) for b in range(BH)]
+        o_dram = [out[b].rearrange("(p n) d -> p n d", n=NT) for b in range(BH)]
+
+        def load_kq(b):
+            nc.sync.dma_start(out=k_sb[b][:], in_=k[b].rearrange("(c p t) d -> p c t d", p=P, t=PACK))
+            nc.sync.dma_start(out=q_sb[b][:], in_=q[b].rearrange("(p n) d -> p n d", n=NT))
+
+        def load_mask(b, n0, n1):
+            nc.sync.dma_start(out=m_sb[b][:, n0:n1, :], in_=m_dram[b][:, n0:n1, :])
+
+        load_kq(0)
+        load_mask(0, 0, 1)
+        load_mask(0, 1, 2)
+        load_mask(0, 2, 4)
+        nc.sync.dma_start(
+            out=v_sb[:],
+            in_=v.flatten_outer_dims().rearrange("(g p t) d -> p g t d", p=P, t=PACK),
+        )
+        load_mask(0, 4, 8)
+        load_kq(1)
+        load_mask(1, 0, 4)
+        load_mask(1, 4, 8)
+
+        ident_bf = const.tile([P, P], BF16, name="ident_bf")
+        make_identity(nc, ident_bf[:])
+        ident_f = const.tile([P, P], F32, name="ident_f")
+        make_identity(nc, ident_f[:])
+
+        n_i = const.tile([P, NBLK], I32, name="n_i")
+        nc.gpsimd.iota(n_i[:], pattern=[[-KPASS, NPASS], [-1, PACK]], base=S - 1, channel_multiplier=-PACK)
+        n_f = const.tile([P, NBLK], F32, name="n_f")
+        nc.vector.tensor_copy(out=n_f[:], in_=n_i[:])
+        y = const.tile([P, NBLK], F32, name="y")
+        nc.scalar.activation(out=y[:], in_=n_f[:], func=ACT.Exp, scale=-LN_A)
+        w = const.tile([P, NBLK], F32, name="w")
+        nc.vector.tensor_scalar(out=w[:], in0=y[:], scalar1=-0.5 * EPS, scalar2=1.0, op0=ALU.mult, op1=ALU.add)
+        dl = const.tile([P, NBLK], F32, name="dl")
+        nc.vector.scalar_tensor_tensor(out=dl[:], in0=y[:], scalar=EPS, in1=w[:], op0=ALU.mult, op1=ALU.mult)
+        lo = const.tile([P, NBLK], F32, name="lo")
+        nc.vector.scalar_tensor_tensor(out=lo[:], in0=n_f[:], scalar=C_LO, in1=dl[:], op0=ALU.mult, op1=ALU.add)
+        ld = const.tile([P, NBLK], F32, name="ld")
+        nc.vector.scalar_tensor_tensor(out=ld[:], in0=n_f[:], scalar=C_HI, in1=lo[:], op0=ALU.mult, op1=ALU.add)
+        ld_rep = const.tile([P, NBLK, P], F32, name="ld_rep")
+        nc.vector.tensor_copy(out=ld_rep[:], in_=ld[:].unsqueeze(2).to_broadcast([P, NBLK, P]))
+
+        kT = [const.tile([P, S], BF16, name="kT%d" % b) for b in range(BH)]
+        qT = [const.tile([P, S], BF16, name="qT%d" % b) for b in range(BH)]
+
+        def transpose_kq(b):
+            kt_ps = ps_t.tile([P, S], BF16, tag="T")
+            for c in range(NPASS):
+                for t in range(PACK):
+                    g = c * PACK + t
+                    nc.tensor.transpose(kt_ps[:, g * P:(g + 1) * P], k_sb[b][:, c, t, :], ident_bf[:])
+            nc.vector.tensor_copy(out=kT[b][:], in_=kt_ps[:])
+            qt_ps = ps_t.tile([P, S], BF16, tag="T")
+            for n in range(NT):
+                nc.tensor.transpose(qt_ps[:, n * P:(n + 1) * P], q_sb[b][:, n, :], ident_bf[:])
+            nc.scalar.copy(out=qT[b][:], in_=qt_ps[:])
+
+        v_grp = const.tile([P, BH * NPASS, D, PACK], BF16, name="v_grp", align_bytes=64)
+        v_codes = const.tile([P, BH * NPASS * D], U32, name="v_codes", align_bytes=64)
+        v_scl = const.tile([P, BH * NPASS * D], U8, name="v_scl", align_bytes=64)
+
+        def quantise_v():
+            nc.vector.tensor_copy(out=v_grp[:], in_=v_sb[:].rearrange("p g t d -> p g d t"))
+            nc.vector.quantize_mx(
+                out=v_codes[:].bitcast(FP8X4),
+                scales=v_scl[:],
+                in_=v_grp[:].rearrange("p g d t -> p (g d t)"),
+            )
+
+        o_sb = [const.tile([P, NT, D], F32, name="o_sb%d" % b) for b in range(BH)]
+
+        def one_tile(b, n):
+            s_sb = work.tile([P, S], F32, name="s_sb")
+            for c in range(NPASS):
+                s_ps = ps_s.tile([P, KPASS], F32, tag="S")
+                for t in range(PACK):
+                    nc.tensor.matmul(
+                        out=s_ps[:, t * P:(t + 1) * P],
+                        lhsT=ld_rep[:, c * PACK + t, :],
+                        rhs=ident_f[:],
+                        is_transpose=True,
+                        start=(t == 0),
+                        stop=False,
+                    )
+                nc.tensor.matmul(
+                    out=s_ps[:],
+                    lhsT=qT[b][:, n * P:(n + 1) * P],
+                    rhs=kT[b][:, c * KPASS:(c + 1) * KPASS],
+                    start=False,
+                    stop=True,
+                )
+                nc.vector.tensor_tensor(
+                    out=s_sb[:, c * KPASS:(c + 1) * KPASS].rearrange("p (t r) -> p t r", t=PACK),
+                    in0=s_ps[:].rearrange("p (t r) -> p t r", t=PACK),
+                    in1=m_sb[b][:, n, c * KPASS:(c + 1) * KPASS].rearrange("p (r t) -> p t r", t=PACK),
+                    op=ALU.add,
+                )
+            negm = small.tile([P, 1], F32, name="negm")
+            nc.vector.tensor_reduce(out=negm[:], in_=s_sb[:], axis=AX.X, op=ALU.max, negate=True)
+            e_bf = work.tile([P, S], BF16, name="e_bf")
+            rsum = small.tile([P, 1], F32, name="rsum")
+            nc.scalar.activation(out=e_bf[:], in_=s_sb[:], func=ACT.Exp, bias=negm[:], scale=1.0, accum_out=rsum[:])
+            e_ps = ps_t.tile([P, S], BF16, tag="T")
+            for g in range(NBLK):
+                nc.tensor.transpose(e_ps[:, g * P:(g + 1) * P], e_bf[:, g * P:(g + 1) * P], ident_bf[:])
+            e_grp = work.tile([P, S], BF16, name="e_grp", align_bytes=64)
+            nc.scalar.copy(
+                out=e_grp[:].rearrange("p (c i t) -> p c i t", c=NPASS, t=PACK),
+                in_=e_ps[:].rearrange("p (c t i) -> p c i t", c=NPASS, t=PACK),
+            )
+            e_codes = work.tile([P, NPASS * P], U32, name="e_codes", align_bytes=64)
+            e_scl = work.tile([P, NPASS * P], U8, name="e_scl", align_bytes=64)
+            nc.vector.quantize_mx(out=e_codes[:].bitcast(FP8X4), scales=e_scl[:], in_=e_grp[:])
+            o_ps = ps_o.tile([P, D], F32, tag="O")
+            for c in range(NPASS):
+                g = b * NPASS + c
+                nc.tensor.matmul_mx(
+                    out=o_ps[:],
+                    lhsT=e_codes[:, c * P:(c + 1) * P].bitcast(FP8X4),
+                    lhsT_scale=e_scl[:, c * P:(c + 1) * P],
+                    rhs=v_codes[:, g * D:(g + 1) * D].bitcast(FP8X4),
+                    rhs_scale=v_scl[:, g * D:(g + 1) * D],
+                    start=(c == 0),
+                    stop=(c == NPASS - 1),
+                )
+            rinv = small.tile([P, 1], F32, name="rinv")
+            nc.vector.reciprocal(out=rinv[:], in_=rsum[:])
+            nc.scalar.activation(out=o_sb[b][:, n, :], in_=o_ps[:], func=ACT.Copy, scale=rinv[:])
+            if n % 2 == 1:
+                nc.sync.dma_start(out=o_dram[b][:, n - 1:n + 1, :], in_=o_sb[b][:, n - 1:n + 1, :])
+
+        transpose_kq(0)
+        quantise_v()
+        for b in range(BH):
+            for n in range(NT):
+                one_tile(b, n)
+                if b == 0 and n == 4:
+                    transpose_kq(1)

@@ -41,6 +41,8 @@ def tile_dotproductattention_kernel(tc, q, k, v, attn_mask, out):
         ps_t = ctx.enter_context(tc.psum_pool(name="ps_t", bufs=2))
         ps_o = ctx.enter_context(tc.psum_pool(name="ps_o", bufs=2))
 
+        ctx.enter_context(tc.manual_schedule())
+
         k_sb = [const.tile([P, NPASS, PACK, D], BF16, name="k_sb%d" % b) for b in range(BH)]
         q_sb = [const.tile([P, NT, D], BF16, name="q_sb%d" % b) for b in range(BH)]
         m_sb = [const.tile([P, NT, S], BF16, name="m_sb%d" % b) for b in range(BH)]
@@ -58,23 +60,23 @@ def tile_dotproductattention_kernel(tc, q, k, v, attn_mask, out):
         load_kq(0)
         load_mask(0, 0, 1)
         load_mask(0, 1, 2)
-        load_mask(0, 2, 4)
         nc.sync.dma_start(
             out=v_sb[:],
             in_=v.flatten_outer_dims().rearrange("(g p t) d -> p g t d", p=P, t=PACK),
         )
-        load_mask(0, 4, 8)
         load_kq(1)
+        load_mask(0, 2, 4)
+        load_mask(0, 4, 8)
         load_mask(1, 0, 4)
         load_mask(1, 4, 8)
 
+        n_i = const.tile([P, NBLK], I32, name="n_i")
+        nc.gpsimd.iota(n_i[:], pattern=[[-KPASS, NPASS], [-1, PACK]], base=S - 1, channel_multiplier=-PACK)
         ident_bf = const.tile([P, P], BF16, name="ident_bf")
         make_identity(nc, ident_bf[:])
         ident_f = const.tile([P, P], F32, name="ident_f")
         make_identity(nc, ident_f[:])
 
-        n_i = const.tile([P, NBLK], I32, name="n_i")
-        nc.gpsimd.iota(n_i[:], pattern=[[-KPASS, NPASS], [-1, PACK]], base=S - 1, channel_multiplier=-PACK)
         n_f = const.tile([P, NBLK], F32, name="n_f")
         nc.vector.tensor_copy(out=n_f[:], in_=n_i[:])
         y = const.tile([P, NBLK], F32, name="y")
@@ -92,40 +94,36 @@ def tile_dotproductattention_kernel(tc, q, k, v, attn_mask, out):
 
         kT = [const.tile([P, S], BF16, name="kT%d" % b) for b in range(BH)]
         qT = [const.tile([P, S], BF16, name="qT%d" % b) for b in range(BH)]
+        v_grp = const.tile([P, BH * NPASS, D, PACK], BF16, name="v_grp", align_bytes=64)
+        v_codes = const.tile([P, BH * NPASS * D], U32, name="v_codes", align_bytes=64)
+        v_scl = const.tile([P, BH * NPASS * D], U8, name="v_scl", align_bytes=64)
+        o_sb = [const.tile([P, NT, D], F32, name="o_sb%d" % b) for b in range(BH)]
 
-        def transpose_kq(b):
+        def transpose_k(b):
             kt_ps = ps_t.tile([P, S], BF16, tag="T")
             for c in range(NPASS):
                 for t in range(PACK):
                     g = c * PACK + t
                     nc.tensor.transpose(kt_ps[:, g * P:(g + 1) * P], k_sb[b][:, c, t, :], ident_bf[:])
-            nc.vector.tensor_copy(out=kT[b][:], in_=kt_ps[:])
+            return kt_ps
+
+        def transpose_q(b):
             qt_ps = ps_t.tile([P, S], BF16, tag="T")
             for n in range(NT):
                 nc.tensor.transpose(qt_ps[:, n * P:(n + 1) * P], q_sb[b][:, n, :], ident_bf[:])
-            nc.scalar.copy(out=qT[b][:], in_=qt_ps[:])
+            return qt_ps
 
-        v_grp = const.tile([P, BH * NPASS, D, PACK], BF16, name="v_grp", align_bytes=64)
-        v_codes = const.tile([P, BH * NPASS * D], U32, name="v_codes", align_bytes=64)
-        v_scl = const.tile([P, BH * NPASS * D], U8, name="v_scl", align_bytes=64)
+        NTILES = BH * NT
+        s_ps, s_sb, negm, e_bf, rsum, rinv, e_ps, e_grp, e_codes, e_scl, o_ps = {}, {}, {}, {}, {}, {}, {}, {}, {}, {}, {}
 
-        def quantise_v():
-            nc.vector.tensor_copy(out=v_grp[:], in_=v_sb[:].rearrange("p g t d -> p g d t"))
-            nc.vector.quantize_mx(
-                out=v_codes[:].bitcast(FP8X4),
-                scales=v_scl[:],
-                in_=v_grp[:].rearrange("p g d t -> p (g d t)"),
-            )
-
-        o_sb = [const.tile([P, NT, D], F32, name="o_sb%d" % b) for b in range(BH)]
-
-        def one_tile(b, n):
-            s_sb = work.tile([P, S], F32, name="s_sb")
+        def stage_scores(i):
+            b, n = divmod(i, NT)
             for c in range(NPASS):
-                s_ps = ps_s.tile([P, KPASS], F32, tag="S")
+                sp = ps_s.tile([P, KPASS], F32, tag="S", name="s_ps")
+                s_ps[(i, c)] = sp
                 for t in range(PACK):
                     nc.tensor.matmul(
-                        out=s_ps[:, t * P:(t + 1) * P],
+                        out=sp[:, t * P:(t + 1) * P],
                         lhsT=ld_rep[:, c * PACK + t, :],
                         rhs=ident_f[:],
                         is_transpose=True,
@@ -133,56 +131,110 @@ def tile_dotproductattention_kernel(tc, q, k, v, attn_mask, out):
                         stop=False,
                     )
                 nc.tensor.matmul(
-                    out=s_ps[:],
+                    out=sp[:],
                     lhsT=qT[b][:, n * P:(n + 1) * P],
                     rhs=kT[b][:, c * KPASS:(c + 1) * KPASS],
                     start=False,
                     stop=True,
                 )
+
+        def stage_mask_max(i):
+            b, n = divmod(i, NT)
+            s_sb[i] = work.tile([P, S], F32, name="s_sb")
+            for c in range(NPASS):
                 nc.vector.tensor_tensor(
-                    out=s_sb[:, c * KPASS:(c + 1) * KPASS].rearrange("p (t r) -> p t r", t=PACK),
-                    in0=s_ps[:].rearrange("p (t r) -> p t r", t=PACK),
+                    out=s_sb[i][:, c * KPASS:(c + 1) * KPASS].rearrange("p (t r) -> p t r", t=PACK),
+                    in0=s_ps[(i, c)][:].rearrange("p (t r) -> p t r", t=PACK),
                     in1=m_sb[b][:, n, c * KPASS:(c + 1) * KPASS].rearrange("p (r t) -> p t r", t=PACK),
                     op=ALU.add,
                 )
-            negm = small.tile([P, 1], F32, name="negm")
-            nc.vector.tensor_reduce(out=negm[:], in_=s_sb[:], axis=AX.X, op=ALU.max, negate=True)
-            e_bf = work.tile([P, S], BF16, name="e_bf")
-            rsum = small.tile([P, 1], F32, name="rsum")
-            nc.scalar.activation(out=e_bf[:], in_=s_sb[:], func=ACT.Exp, bias=negm[:], scale=1.0, accum_out=rsum[:])
-            e_ps = ps_t.tile([P, S], BF16, tag="T")
-            for g in range(NBLK):
-                nc.tensor.transpose(e_ps[:, g * P:(g + 1) * P], e_bf[:, g * P:(g + 1) * P], ident_bf[:])
-            e_grp = work.tile([P, S], BF16, name="e_grp", align_bytes=64)
-            nc.scalar.copy(
-                out=e_grp[:].rearrange("p (c i t) -> p c i t", c=NPASS, t=PACK),
-                in_=e_ps[:].rearrange("p (c t i) -> p c i t", c=NPASS, t=PACK),
+            negm[i] = small.tile([P, 1], F32, name="negm")
+            nc.vector.tensor_reduce(out=negm[i][:], in_=s_sb[i][:], axis=AX.X, op=ALU.max, negate=True)
+
+        def stage_exp(i):
+            e_bf[i] = work.tile([P, S], BF16, name="e_bf")
+            if i % 2 == 0:
+                rsum[i // 2] = small.tile([P, 2], F32, name="rsum")
+            nc.scalar.activation(
+                out=e_bf[i][:], in_=s_sb[i][:], func=ACT.Exp, bias=negm[i][:], scale=1.0,
+                accum_out=rsum[i // 2][:, i % 2:i % 2 + 1],
             )
-            e_codes = work.tile([P, NPASS * P], U32, name="e_codes", align_bytes=64)
-            e_scl = work.tile([P, NPASS * P], U8, name="e_scl", align_bytes=64)
-            nc.vector.quantize_mx(out=e_codes[:].bitcast(FP8X4), scales=e_scl[:], in_=e_grp[:])
-            o_ps = ps_o.tile([P, D], F32, tag="O")
+
+        def stage_transpose(i):
+            e_ps[i] = ps_t.tile([P, S], BF16, tag="T", name="e_ps")
+            for g in range(NBLK):
+                nc.tensor.transpose(e_ps[i][:, g * P:(g + 1) * P], e_bf[i][:, g * P:(g + 1) * P], ident_bf[:])
+
+        def stage_group(i, on_vector):
+            e_grp[i] = work.tile([P, S], BF16, name="e_grp", align_bytes=64)
+            dst = e_grp[i][:].rearrange("p (c i t) -> p c i t", c=NPASS, t=PACK)
+            src = e_ps[i][:].rearrange("p (c t i) -> p c i t", c=NPASS, t=PACK)
+            if on_vector:
+                nc.vector.tensor_copy(out=dst, in_=src)
+            else:
+                nc.scalar.copy(out=dst, in_=src)
+
+        def stage_quantise(i):
+            e_codes[i] = work.tile([P, NPASS * P], U32, name="e_codes", align_bytes=64)
+            e_scl[i] = work.tile([P, NPASS * P], U8, name="e_scl", align_bytes=64)
+            nc.vector.quantize_mx(out=e_codes[i][:].bitcast(FP8X4), scales=e_scl[i][:], in_=e_grp[i][:])
+            if i % 2 == 0:
+                rinv[i // 2] = small.tile([P, 2], F32, name="rinv")
+                nc.vector.reciprocal(out=rinv[i // 2][:], in_=rsum[i // 2][:])
+
+        def stage_pv(i):
+            b = i // NT
+            o_ps[i] = ps_o.tile([P, D], F32, tag="O", name="o_ps")
             for c in range(NPASS):
                 g = b * NPASS + c
                 nc.tensor.matmul_mx(
-                    out=o_ps[:],
-                    lhsT=e_codes[:, c * P:(c + 1) * P].bitcast(FP8X4),
-                    lhsT_scale=e_scl[:, c * P:(c + 1) * P],
+                    out=o_ps[i][:],
+                    lhsT=e_codes[i][:, c * P:(c + 1) * P].bitcast(FP8X4),
+                    lhsT_scale=e_scl[i][:, c * P:(c + 1) * P],
                     rhs=v_codes[:, g * D:(g + 1) * D].bitcast(FP8X4),
                     rhs_scale=v_scl[:, g * D:(g + 1) * D],
                     start=(c == 0),
                     stop=(c == NPASS - 1),
                 )
-            rinv = small.tile([P, 1], F32, name="rinv")
-            nc.vector.reciprocal(out=rinv[:], in_=rsum[:])
-            nc.scalar.activation(out=o_sb[b][:, n, :], in_=o_ps[:], func=ACT.Copy, scale=rinv[:])
+
+        def stage_out(i):
+            b, n = divmod(i, NT)
+            nc.scalar.activation(
+                out=o_sb[b][:, n, :], in_=o_ps[i][:], func=ACT.Copy, scale=rinv[i // 2][:, i % 2:i % 2 + 1]
+            )
             if n % 2 == 1:
                 nc.sync.dma_start(out=o_dram[b][:, n - 1:n + 1, :], in_=o_sb[b][:, n - 1:n + 1, :])
 
-        transpose_kq(0)
-        quantise_v()
-        for b in range(BH):
-            for n in range(NT):
-                one_tile(b, n)
-                if b == 0 and n == 4:
-                    transpose_kq(1)
+        kt0 = transpose_k(0)
+        nc.vector.tensor_copy(out=kT[0][:], in_=kt0[:])
+        qt0 = transpose_q(0)
+        nc.scalar.copy(out=qT[0][:], in_=qt0[:])
+        nc.scalar.copy(out=v_grp[:], in_=v_sb[:].rearrange("p g t d -> p g d t"))
+        late = {}
+        for step in range(-1, NTILES + 3):
+            if step + 1 < NTILES:
+                stage_scores(step + 1)
+            if step == 0:
+                late["k"] = transpose_k(1)
+                late["q"] = transpose_q(1)
+            if step == 1:
+                nc.vector.tensor_copy(out=kT[1][:], in_=late["k"][:])
+            if step == 2:
+                nc.vector.tensor_copy(out=qT[1][:], in_=late["q"][:])
+                nc.vector.quantize_mx(
+                    out=v_codes[:].bitcast(FP8X4),
+                    scales=v_scl[:],
+                    in_=v_grp[:].rearrange("p g d t -> p (g d t)"),
+                )
+            if 0 <= step - 3:
+                stage_quantise(step - 3)
+                stage_pv(step - 3)
+            if 0 <= step < NTILES:
+                stage_mask_max(step)
+            if 0 <= step - 1 < NTILES:
+                stage_exp(step - 1)
+                stage_transpose(step - 1)
+            if 0 <= step - 2 < NTILES:
+                stage_group(step - 2, step - 2 >= NTILES - 2)
+            if 0 <= step - 3:
+                stage_out(step - 3)

@@ -90,7 +90,9 @@ def tile_dotproductattention_kernel(tc, q, k, v, attn_mask, out):
         ld = const.tile([P, NBLK], F32, name="ld")
         nc.vector.scalar_tensor_tensor(out=ld[:], in0=n_f[:], scalar=C_HI, in1=lo[:], op0=ALU.mult, op1=ALU.add)
         ld_rep = const.tile([P, NBLK, P], F32, name="ld_rep")
-        nc.vector.tensor_copy(out=ld_rep[:], in_=ld[:].unsqueeze(2).to_broadcast([P, NBLK, P]))
+        for c in range(NPASS):
+            blk = slice(c * PACK, (c + 1) * PACK)
+            nc.vector.tensor_copy(out=ld_rep[:, blk, :], in_=ld[:, blk].unsqueeze(2).to_broadcast([P, PACK, P]))
 
         kT = [const.tile([P, S], BF16, name="kT%d" % b) for b in range(BH)]
         qT = [const.tile([P, S], BF16, name="qT%d" % b) for b in range(BH)]
@@ -107,13 +109,14 @@ def tile_dotproductattention_kernel(tc, q, k, v, attn_mask, out):
                     nc.tensor.transpose(kt_ps[:, g * P:(g + 1) * P], k_sb[b][:, c, t, :], ident_bf[:])
             return kt_ps
 
-        def transpose_q(b):
-            qt_ps = ps_t.tile([P, S], BF16, tag="T")
-            for n in range(NT):
-                nc.tensor.transpose(qt_ps[:, n * P:(n + 1) * P], q_sb[b][:, n, :], ident_bf[:])
+        def transpose_q(b, n0, n1, pool, tag):
+            qt_ps = pool.tile([P, (n1 - n0) * P], BF16, tag=tag)
+            for n in range(n0, n1):
+                nc.tensor.transpose(qt_ps[:, (n - n0) * P:(n - n0 + 1) * P], q_sb[b][:, n, :], ident_bf[:])
             return qt_ps
 
         NTILES = BH * NT
+        LAST = NTILES - 1
         s_ps, s_sb, negm, e_bf, rsum, rinv, e_ps, e_grp, e_codes, e_scl, o_ps = {}, {}, {}, {}, {}, {}, {}, {}, {}, {}, {}
 
         def stage_scores(i):
@@ -135,8 +138,23 @@ def tile_dotproductattention_kernel(tc, q, k, v, attn_mask, out):
                     lhsT=qT[b][:, n * P:(n + 1) * P],
                     rhs=kT[b][:, c * KPASS:(c + 1) * KPASS],
                     start=False,
-                    stop=True,
+                    stop=(i != LAST),
                 )
+                if i == LAST:
+                    nc.tensor.matmul(
+                        out=sp[:].rearrange("p (t r) -> p t r", t=PACK),
+                        lhsT=ident_bf[:],
+                        rhs=m_sb[b][:, n, c * KPASS:(c + 1) * KPASS].rearrange("p (r t) -> p t r", t=PACK),
+                        start=False,
+                        stop=True,
+                    )
+
+        def stage_max_last():
+            pm = small.tile([P, NPASS], F32, name="pm")
+            for c in range(NPASS):
+                nc.vector.tensor_reduce(out=pm[:, c:c + 1], in_=s_ps[(LAST, c)][:], axis=AX.X, op=ALU.max)
+            negm[LAST] = small.tile([P, 1], F32, name="negm")
+            nc.vector.tensor_reduce(out=negm[LAST][:], in_=pm[:], axis=AX.X, op=ALU.max, negate=True)
 
         def stage_mask_max(i):
             b, n = divmod(i, NT)
@@ -179,8 +197,9 @@ def tile_dotproductattention_kernel(tc, q, k, v, attn_mask, out):
             e_scl[i] = work.tile([P, NPASS * P], U8, name="e_scl", align_bytes=64)
             nc.vector.quantize_mx(out=e_codes[i][:].bitcast(FP8X4), scales=e_scl[i][:], in_=e_grp[i][:])
             if i % 2 == 0:
+                cols = 1 if i == LAST - 1 else 2
                 rinv[i // 2] = small.tile([P, 2], F32, name="rinv")
-                nc.vector.reciprocal(out=rinv[i // 2][:], in_=rsum[i // 2][:])
+                nc.vector.reciprocal(out=rinv[i // 2][:, 0:cols], in_=rsum[i // 2][:, 0:cols])
 
         def stage_pv(i):
             b = i // NT
@@ -202,25 +221,30 @@ def tile_dotproductattention_kernel(tc, q, k, v, attn_mask, out):
             nc.scalar.activation(
                 out=o_sb[b][:, n, :], in_=o_ps[i][:], func=ACT.Copy, scale=rinv[i // 2][:, i % 2:i % 2 + 1]
             )
-            if n % 2 == 1:
+            if i == LAST - 1:
+                nc.sync.dma_start(out=o_dram[b][:, n:n + 1, :], in_=o_sb[b][:, n:n + 1, :])
+            elif n % 2 == 1:
                 nc.sync.dma_start(out=o_dram[b][:, n - 1:n + 1, :], in_=o_sb[b][:, n - 1:n + 1, :])
 
         kt0 = transpose_k(0)
         nc.vector.tensor_copy(out=kT[0][:], in_=kt0[:])
-        qt0 = transpose_q(0)
-        nc.scalar.copy(out=qT[0][:], in_=qt0[:])
-        nc.scalar.copy(out=v_grp[:], in_=v_sb[:].rearrange("p g t d -> p g d t"))
+        qa = transpose_q(0, 0, 2, ps_o, "O")
+        nc.scalar.copy(out=qT[0][:, 0:2 * P], in_=qa[:])
+        stage_scores(0)
+        qb = transpose_q(0, 2, NT, ps_t, "T")
+        nc.scalar.copy(out=qT[0][:, 2 * P:S], in_=qb[:])
+        nc.gpsimd.tensor_scalar(
+            out=v_grp[:], in0=v_sb[:].rearrange("p g t d -> p g d t"),
+            scalar1=1.0, scalar2=0.0, op0=ALU.mult, op1=ALU.add,
+        )
         late = {}
-        for step in range(-1, NTILES + 3):
+        for step in range(0, NTILES):
             if step + 1 < NTILES:
                 stage_scores(step + 1)
             if step == 0:
                 late["k"] = transpose_k(1)
-                late["q"] = transpose_q(1)
-            if step == 1:
-                nc.vector.tensor_copy(out=kT[1][:], in_=late["k"][:])
+                late["q"] = transpose_q(1, 0, NT, ps_t, "T")
             if step == 2:
-                nc.vector.tensor_copy(out=qT[1][:], in_=late["q"][:])
                 nc.vector.quantize_mx(
                     out=v_codes[:].bitcast(FP8X4),
                     scales=v_scl[:],
@@ -229,12 +253,81 @@ def tile_dotproductattention_kernel(tc, q, k, v, attn_mask, out):
             if 0 <= step - 3:
                 stage_quantise(step - 3)
                 stage_pv(step - 3)
-            if 0 <= step < NTILES:
+            if step == LAST:
+                stage_max_last()
+            else:
                 stage_mask_max(step)
-            if 0 <= step - 1 < NTILES:
+            if 0 <= step - 1:
                 stage_exp(step - 1)
+                if step == 1:
+                    nc.scalar.copy(out=kT[1][:], in_=late["k"][:])
+                    nc.scalar.copy(out=qT[1][:], in_=late["q"][:])
                 stage_transpose(step - 1)
-            if 0 <= step - 2 < NTILES:
-                stage_group(step - 2, step - 2 >= NTILES - 2)
+            if 0 <= step - 2:
+                stage_group(step - 2, False)
             if 0 <= step - 3:
                 stage_out(step - 3)
+
+        b, n = divmod(LAST, NT)
+        rs_h = small.tile([P, NPASS], F32, name="rs_h")
+        eh_bf, eh_ps, eh_grp, eh_codes, eh_scl = {}, {}, {}, {}, {}
+
+        def exp_half(c):
+            eh_bf[c] = work.tile([P, KPASS], BF16, name="eh_bf")
+            nc.scalar.activation(
+                out=eh_bf[c][:], in_=s_ps[(LAST, c)][:], func=ACT.Exp, bias=negm[LAST][:], scale=1.0,
+                accum_out=rs_h[:, c:c + 1],
+            )
+
+        def transpose_half(c):
+            eh_ps[c] = ps_t.tile([P, KPASS], BF16, tag="T", name="eh_ps")
+            for t in range(PACK):
+                nc.tensor.transpose(eh_ps[c][:, t * P:(t + 1) * P], eh_bf[c][:, t * P:(t + 1) * P], ident_bf[:])
+
+        def group_half(c, on_vector):
+            eh_grp[c] = work.tile([P, KPASS], BF16, name="eh_grp", align_bytes=64)
+            dst = eh_grp[c][:].rearrange("p (i t) -> p i t", t=PACK)
+            src = eh_ps[c][:].rearrange("p (t i) -> p i t", t=PACK)
+            if on_vector:
+                nc.vector.tensor_copy(out=dst, in_=src)
+            else:
+                nc.scalar.copy(out=dst, in_=src)
+
+        def quantise_half(c):
+            eh_codes[c] = work.tile([P, P], U32, name="eh_codes", align_bytes=64)
+            eh_scl[c] = work.tile([P, P], U8, name="eh_scl", align_bytes=64)
+            nc.vector.quantize_mx(out=eh_codes[c][:].bitcast(FP8X4), scales=eh_scl[c][:], in_=eh_grp[c][:])
+
+        stage_quantise(LAST - 2)
+        stage_pv(LAST - 2)
+        exp_half(0)
+        transpose_half(0)
+        stage_group(LAST - 1, True)
+        exp_half(1)
+        stage_quantise(LAST - 1)
+        transpose_half(1)
+        stage_out(LAST - 2)
+        stage_pv(LAST - 1)
+        group_half(0, True)
+        group_half(1, False)
+        stage_out(LAST - 1)
+        rs_t = small.tile([P, 1], F32, name="rs_t")
+        nc.vector.tensor_reduce(out=rs_t[:], in_=rs_h[:], axis=AX.X, op=ALU.add)
+        ri_t = small.tile([P, 1], F32, name="ri_t")
+        nc.vector.reciprocal(out=ri_t[:], in_=rs_t[:])
+        quantise_half(0)
+        quantise_half(1)
+        o_last = ps_o.tile([P, D], F32, tag="O", name="o_last")
+        for c in range(NPASS):
+            g = b * NPASS + c
+            nc.tensor.matmul_mx(
+                out=o_last[:],
+                lhsT=eh_codes[c][:].bitcast(FP8X4),
+                lhsT_scale=eh_scl[c][:],
+                rhs=v_codes[:, g * D:(g + 1) * D].bitcast(FP8X4),
+                rhs_scale=v_scl[:, g * D:(g + 1) * D],
+                start=(c == 0),
+                stop=(c == NPASS - 1),
+            )
+        nc.scalar.activation(out=o_sb[b][:, n, :], in_=o_last[:], func=ACT.Copy, scale=ri_t[:])
+        nc.sync.dma_start(out=o_dram[b][:, n:n + 1, :], in_=o_sb[b][:, n:n + 1, :])

@@ -156,7 +156,7 @@ def tile_dotproductattention_kernel(tc, q, k, v, attn_mask, out):
             negm[LAST] = small.tile([P, 1], F32, name="negm")
             nc.vector.tensor_reduce(out=negm[LAST][:], in_=pm[:], axis=AX.X, op=ALU.max, negate=True)
 
-        def stage_mask_max(i):
+        def stage_mask(i):
             b, n = divmod(i, NT)
             s_sb[i] = work.tile([P, S], F32, name="s_sb")
             for c in range(NPASS):
@@ -166,6 +166,8 @@ def tile_dotproductattention_kernel(tc, q, k, v, attn_mask, out):
                     in1=m_sb[b][:, n, c * KPASS:(c + 1) * KPASS].rearrange("p (r t) -> p t r", t=PACK),
                     op=ALU.add,
                 )
+
+        def stage_max(i):
             negm[i] = small.tile([P, 1], F32, name="negm")
             nc.vector.tensor_reduce(out=negm[i][:], in_=s_sb[i][:], axis=AX.X, op=ALU.max, negate=True)
 
@@ -250,13 +252,15 @@ def tile_dotproductattention_kernel(tc, q, k, v, attn_mask, out):
                     scales=v_scl[:],
                     in_=v_grp[:].rearrange("p g d t -> p (g d t)"),
                 )
+            if step != LAST:
+                stage_mask(step)
             if 0 <= step - 3:
                 stage_quantise(step - 3)
                 stage_pv(step - 3)
             if step == LAST:
                 stage_max_last()
             else:
-                stage_mask_max(step)
+                stage_max(step)
             if 0 <= step - 1:
                 stage_exp(step - 1)
                 if step == 1:

@@ -267,7 +267,7 @@ def tile_dotproductattention_kernel(tc, q, k, v, attn_mask, out):
                     nc.scalar.copy(out=kT[1][:], in_=late["k"][:])
                     nc.scalar.copy(out=qT[1][:], in_=late["q"][:])
                 stage_transpose(step - 1)
-            if 0 <= step - 2:
+            if 0 <= step - 2 < LAST - 2:
                 stage_group(step - 2, False)
             if 0 <= step - 3:
                 stage_out(step - 3)
@@ -284,7 +284,7 @@ def tile_dotproductattention_kernel(tc, q, k, v, attn_mask, out):
             )
 
         def transpose_half(c):
-            eh_ps[c] = ps_t.tile([P, KPASS], BF16, tag="T", name="eh_ps")
+            eh_ps[c] = ps_s.tile([P, KPASS], BF16, tag="S", name="eh_ps")
             for t in range(PACK):
                 nc.tensor.transpose(eh_ps[c][:, t * P:(t + 1) * P], eh_bf[c][:, t * P:(t + 1) * P], ident_bf[:])
 
@@ -302,25 +302,26 @@ def tile_dotproductattention_kernel(tc, q, k, v, attn_mask, out):
             eh_scl[c] = work.tile([P, P], U8, name="eh_scl", align_bytes=64)
             nc.vector.quantize_mx(out=eh_codes[c][:].bitcast(FP8X4), scales=eh_scl[c][:], in_=eh_grp[c][:])
 
-        stage_quantise(LAST - 2)
-        stage_pv(LAST - 2)
         exp_half(0)
         transpose_half(0)
-        stage_group(LAST - 1, True)
         exp_half(1)
-        stage_quantise(LAST - 1)
         transpose_half(1)
-        stage_out(LAST - 2)
-        stage_pv(LAST - 1)
-        group_half(0, True)
+        stage_group(LAST - 2, True)
+        stage_group(LAST - 1, True)
+        stage_quantise(LAST - 2)
+        stage_pv(LAST - 2)
+        group_half(0, False)
         group_half(1, False)
-        stage_out(LAST - 1)
+        stage_out(LAST - 2)
+        stage_quantise(LAST - 1)
+        stage_pv(LAST - 1)
         rs_t = small.tile([P, 1], F32, name="rs_t")
         nc.vector.tensor_reduce(out=rs_t[:], in_=rs_h[:], axis=AX.X, op=ALU.add)
         ri_t = small.tile([P, 1], F32, name="ri_t")
         nc.vector.reciprocal(out=ri_t[:], in_=rs_t[:])
         quantise_half(0)
         quantise_half(1)
+        stage_out(LAST - 1)
         o_last = ps_o.tile([P, D], F32, tag="O", name="o_last")
         for c in range(NPASS):
             g = b * NPASS + c

@@ -29,6 +29,8 @@ C_HI = round(LN_A * 2.0 ** 20) / 2.0 ** 20
 C_LO = LN_A - C_HI
 
 FLOPS = 2 * 2 * BH * S * S * D
+WARM = 5
+WARM_N = 256
 
 
 def tile_dotproductattention_kernel(tc, q, k, v, attn_mask, out):
@@ -70,6 +72,11 @@ def tile_dotproductattention_kernel(tc, q, k, v, attn_mask, out):
         load_mask(1, 0, 4)
         load_mask(1, 4, 8)
 
+        warm_in = const.tile([P, PACK * WARM_N], BF16, name="warm_in", align_bytes=64)
+        nc.vector.memset(warm_in[:].bitcast(I32), 0)
+        warm_w = const.tile([P, WARM_N], U32, name="warm_w", align_bytes=64)
+        warm_s = const.tile([P, WARM_N], U8, name="warm_s", align_bytes=64)
+
         n_i = const.tile([P, NBLK], I32, name="n_i")
         nc.gpsimd.iota(n_i[:], pattern=[[-KPASS, NPASS], [-1, PACK]], base=S - 1, channel_multiplier=-PACK)
         ident_bf = const.tile([P, P], BF16, name="ident_bf")
@@ -79,6 +86,18 @@ def tile_dotproductattention_kernel(tc, q, k, v, attn_mask, out):
 
         n_f = const.tile([P, NBLK], F32, name="n_f")
         nc.vector.tensor_copy(out=n_f[:], in_=n_i[:])
+        nc.vector.quantize_mx(out=warm_w[:].bitcast(FP8X4), scales=warm_s[:], in_=warm_in[:])
+        warm_ps = ps_s.tile([P, WARM_N], F32, tag="S", name="warm_ps")
+        for r in range(WARM):
+            nc.tensor.matmul_mx(
+                out=warm_ps[:],
+                lhsT=warm_w[:, 0:P].bitcast(FP8X4),
+                lhsT_scale=warm_s[:, 0:P],
+                rhs=warm_w[:].bitcast(FP8X4),
+                rhs_scale=warm_s[:],
+                start=True,
+                stop=True,
+            )
         y = const.tile([P, NBLK], F32, name="y")
         nc.scalar.activation(out=y[:], in_=n_f[:], func=ACT.Exp, scale=-LN_A)
         w = const.tile([P, NBLK], F32, name="w")

@@ -21,6 +21,8 @@ PACK = 4
 KPASS = P * PACK
 NPASS = S // KPASS
 NBLK = NPASS * PACK
+HALF = 2
+NWORD = NPASS * HALF
 
 ALPHA = 0.99
 EPS = 1e-10
@@ -45,15 +47,15 @@ def tile_dotproductattention_kernel(tc, q, k, v, attn_mask, out):
 
         ctx.enter_context(tc.manual_schedule())
 
-        k_sb = [const.tile([P, NPASS, PACK, D], BF16, name="k_sb%d" % b) for b in range(BH)]
+        k_sb = [const.tile([P, NPASS * HALF, 2, D], BF16, name="k_sb%d" % b) for b in range(BH)]
         q_sb = [const.tile([P, NT, D], BF16, name="q_sb%d" % b) for b in range(BH)]
         m_sb = [const.tile([P, NT, S], BF16, name="m_sb%d" % b) for b in range(BH)]
-        v_sb = const.tile([P, BH * NPASS, PACK, D], BF16, name="v_sb")
+        v_sb = const.tile([P, BH * NWORD, 2, D], BF16, name="v_sb")
         m_dram = [attn_mask[b].rearrange("(p n) j -> p n j", n=NT) for b in range(BH)]
         o_dram = [out[b].rearrange("(p n) d -> p n d", n=NT) for b in range(BH)]
 
         def load_kq(b):
-            nc.sync.dma_start(out=k_sb[b][:], in_=k[b].rearrange("(c p t) d -> p c t d", p=P, t=PACK))
+            nc.sync.dma_start(out=k_sb[b][:], in_=k[b].rearrange("(w p e) d -> p w e d", p=P, e=2))
             nc.sync.dma_start(out=q_sb[b][:], in_=q[b].rearrange("(p n) d -> p n d", n=NT))
 
         def load_mask(b, n0, n1):
@@ -64,7 +66,7 @@ def tile_dotproductattention_kernel(tc, q, k, v, attn_mask, out):
         load_mask(0, 1, 2)
         nc.sync.dma_start(
             out=v_sb[:],
-            in_=v.flatten_outer_dims().rearrange("(g p t) d -> p g t d", p=P, t=PACK),
+            in_=v.flatten_outer_dims().rearrange("(w p e) d -> p w e d", p=P, e=2),
         )
         load_kq(1)
         load_mask(0, 2, 4)
@@ -78,7 +80,7 @@ def tile_dotproductattention_kernel(tc, q, k, v, attn_mask, out):
         warm_s = const.tile([P, WARM_N], U8, name="warm_s", align_bytes=64)
 
         n_i = const.tile([P, NBLK], I32, name="n_i")
-        nc.gpsimd.iota(n_i[:], pattern=[[-KPASS, NPASS], [-1, PACK]], base=S - 1, channel_multiplier=-PACK)
+        nc.gpsimd.iota(n_i[:], pattern=[[-2 * P, NWORD], [-1, 2]], base=S - 1, channel_multiplier=-2)
         ident_bf = const.tile([P, P], BF16, name="ident_bf")
         make_identity(nc, ident_bf[:])
         ident_f = const.tile([P, P], F32, name="ident_f")
@@ -122,10 +124,10 @@ def tile_dotproductattention_kernel(tc, q, k, v, attn_mask, out):
 
         def transpose_k(b):
             kt_ps = ps_t.tile([P, S], BF16, tag="T")
-            for c in range(NPASS):
-                for t in range(PACK):
-                    g = c * PACK + t
-                    nc.tensor.transpose(kt_ps[:, g * P:(g + 1) * P], k_sb[b][:, c, t, :], ident_bf[:])
+            for w_ in range(NWORD):
+                for e in range(2):
+                    g = 2 * w_ + e
+                    nc.tensor.transpose(kt_ps[:, g * P:(g + 1) * P], k_sb[b][:, w_, e, :], ident_bf[:])
             return kt_ps
 
         def transpose_q(b, n0, n1, pool, tag):
@@ -161,9 +163,9 @@ def tile_dotproductattention_kernel(tc, q, k, v, attn_mask, out):
                 )
                 if i == LAST:
                     nc.tensor.matmul(
-                        out=sp[:].rearrange("p (t r) -> p t r", t=PACK),
+                        out=sp[:].rearrange("p (u e r) -> p u e r", u=HALF, e=2),
                         lhsT=ident_bf[:],
-                        rhs=m_sb[b][:, n, c * KPASS:(c + 1) * KPASS].rearrange("p (r t) -> p t r", t=PACK),
+                        rhs=m_sb[b][:, n, c * KPASS:(c + 1) * KPASS].rearrange("p (u r e) -> p u e r", u=HALF, e=2),
                         start=False,
                         stop=True,
                     )
@@ -180,9 +182,9 @@ def tile_dotproductattention_kernel(tc, q, k, v, attn_mask, out):
             s_sb[i] = work.tile([P, S], F32, name="s_sb")
             for c in range(NPASS):
                 nc.vector.tensor_tensor(
-                    out=s_sb[i][:, c * KPASS:(c + 1) * KPASS].rearrange("p (t r) -> p t r", t=PACK),
-                    in0=s_ps[(i, c)][:].rearrange("p (t r) -> p t r", t=PACK),
-                    in1=m_sb[b][:, n, c * KPASS:(c + 1) * KPASS].rearrange("p (r t) -> p t r", t=PACK),
+                    out=s_sb[i][:, c * KPASS:(c + 1) * KPASS].rearrange("p (u r e) -> p u r e", u=HALF, e=2),
+                    in0=s_ps[(i, c)][:].rearrange("p (u e r) -> p u r e", u=HALF, e=2),
+                    in1=m_sb[b][:, n, c * KPASS:(c + 1) * KPASS].rearrange("p (u r e) -> p u r e", u=HALF, e=2),
                     op=ALU.add,
                 )
 
@@ -200,14 +202,15 @@ def tile_dotproductattention_kernel(tc, q, k, v, attn_mask, out):
             )
 
         def stage_transpose(i):
-            e_ps[i] = ps_t.tile([P, S], BF16, tag="T", name="e_ps")
-            for g in range(NBLK):
-                nc.tensor.transpose(e_ps[i][:, g * P:(g + 1) * P], e_bf[i][:, g * P:(g + 1) * P], ident_bf[:])
+            e_ps[i] = ps_t.tile([P, NWORD * P], F32, tag="T", name="e_ps")
+            words = e_bf[i][:].bitcast(F32)
+            for g in range(NWORD):
+                nc.tensor.transpose(e_ps[i][:, g * P:(g + 1) * P], words[:, g * P:(g + 1) * P], ident_f[:])
 
         def stage_group(i, on_vector):
             e_grp[i] = work.tile([P, S], BF16, name="e_grp", align_bytes=64)
-            dst = e_grp[i][:].rearrange("p (c i t) -> p c i t", c=NPASS, t=PACK)
-            src = e_ps[i][:].rearrange("p (c t i) -> p c i t", c=NPASS, t=PACK)
+            dst = e_grp[i][:].bitcast(F32).rearrange("p (c i u) -> p c i u", c=NPASS, u=HALF)
+            src = e_ps[i][:].rearrange("p (c u i) -> p c i u", c=NPASS, u=HALF)
             if on_vector:
                 nc.vector.tensor_copy(out=dst, in_=src)
             else:
@@ -255,7 +258,7 @@ def tile_dotproductattention_kernel(tc, q, k, v, attn_mask, out):
         qb = transpose_q(0, 2, NT, ps_t, "T")
         nc.scalar.copy(out=qT[0][:, 2 * P:S], in_=qb[:])
         nc.gpsimd.tensor_scalar(
-            out=v_grp[:], in0=v_sb[:].rearrange("p g t d -> p g d t"),
+            out=v_grp[:], in0=v_sb[:].rearrange("p (g u) e d -> p g d (u e)", u=HALF),
             scalar1=1.0, scalar2=0.0, op0=ALU.mult, op1=ALU.add,
         )
         late = {}
@@ -298,19 +301,22 @@ def tile_dotproductattention_kernel(tc, q, k, v, attn_mask, out):
         def exp_half(c):
             eh_bf[c] = work.tile([P, KPASS], BF16, name="eh_bf")
             nc.scalar.activation(
-                out=eh_bf[c][:], in_=s_ps[(LAST, c)][:], func=ACT.Exp, bias=negm[LAST][:], scale=1.0,
+                out=eh_bf[c][:].rearrange("p (u r e) -> p u r e", u=HALF, e=2),
+                in_=s_ps[(LAST, c)][:].rearrange("p (u e r) -> p u r e", u=HALF, e=2),
+                func=ACT.Exp, bias=negm[LAST][:], scale=1.0,
                 accum_out=rs_h[:, c:c + 1],
             )
 
         def transpose_half(c):
-            eh_ps[c] = ps_s.tile([P, KPASS], BF16, tag="S", name="eh_ps")
-            for t in range(PACK):
-                nc.tensor.transpose(eh_ps[c][:, t * P:(t + 1) * P], eh_bf[c][:, t * P:(t + 1) * P], ident_bf[:])
+            eh_ps[c] = ps_s.tile([P, HALF * P], F32, tag="S", name="eh_ps")
+            words = eh_bf[c][:].bitcast(F32)
+            for u in range(HALF):
+                nc.tensor.transpose(eh_ps[c][:, u * P:(u + 1) * P], words[:, u * P:(u + 1) * P], ident_f[:])
 
         def group_half(c, on_vector):
             eh_grp[c] = work.tile([P, KPASS], BF16, name="eh_grp", align_bytes=64)
-            dst = eh_grp[c][:].rearrange("p (i t) -> p i t", t=PACK)
-            src = eh_ps[c][:].rearrange("p (t i) -> p i t", t=PACK)
+            dst = eh_grp[c][:].bitcast(F32).rearrange("p (i u) -> p i u", u=HALF)
+            src = eh_ps[c][:].rearrange("p (u i) -> p i u", u=HALF)
             if on_vector:
                 nc.vector.tensor_copy(out=dst, in_=src)
             else:

@@ -33,13 +33,18 @@ C_LO = LN_A - C_HI
 FLOPS = 2 * 2 * BH * S * S * D
 WARM = 5
 WARM_N = 256
+SPLIT = 4
+
+
+def on_gpsimd(i):
+    return i > 1 and i % 4 == 1
 
 
 def tile_dotproductattention_kernel(tc, q, k, v, attn_mask, out):
     nc = tc.nc
     with ExitStack() as ctx:
         const = ctx.enter_context(tc.tile_pool(name="const", bufs=1))
-        work = ctx.enter_context(tc.tile_pool(name="work", bufs=3))
+        work = ctx.enter_context(tc.tile_pool(name="work", bufs=4))
         small = ctx.enter_context(tc.tile_pool(name="small", bufs=4))
         ps_s = ctx.enter_context(tc.psum_pool(name="ps_s", bufs=4))
         ps_t = ctx.enter_context(tc.psum_pool(name="ps_t", bufs=2))
@@ -140,57 +145,69 @@ def tile_dotproductattention_kernel(tc, q, k, v, attn_mask, out):
         LAST = NTILES - 1
         s_ps, s_sb, negm, e_bf, rsum, rinv, e_ps, e_grp, e_codes, e_scl, o_ps = {}, {}, {}, {}, {}, {}, {}, {}, {}, {}, {}
 
-        def stage_scores(i):
+        def scores(i, c):
             b, n = divmod(i, NT)
-            for c in range(NPASS):
-                sp = ps_s.tile([P, KPASS], F32, tag="S", name="s_ps")
-                s_ps[(i, c)] = sp
-                for t in range(PACK):
-                    nc.tensor.matmul(
-                        out=sp[:, t * P:(t + 1) * P],
-                        lhsT=ld_rep[:, c * PACK + t, :],
-                        rhs=ident_f[:],
-                        is_transpose=True,
-                        start=(t == 0),
-                        stop=False,
-                    )
+            sp = ps_s.tile([P, KPASS], F32, tag="S", name="s_ps")
+            s_ps[(i, c)] = sp
+            for t in range(PACK):
                 nc.tensor.matmul(
-                    out=sp[:],
-                    lhsT=qT[b][:, n * P:(n + 1) * P],
-                    rhs=kT[b][:, c * KPASS:(c + 1) * KPASS],
-                    start=False,
-                    stop=(i != LAST),
+                    out=sp[:, t * P:(t + 1) * P],
+                    lhsT=ld_rep[:, c * PACK + t, :],
+                    rhs=ident_f[:],
+                    is_transpose=True,
+                    start=(t == 0),
+                    stop=False,
                 )
-                if i == LAST:
-                    nc.tensor.matmul(
-                        out=sp[:].rearrange("p (u e r) -> p u e r", u=HALF, e=2),
-                        lhsT=ident_bf[:],
-                        rhs=m_sb[b][:, n, c * KPASS:(c + 1) * KPASS].rearrange("p (u r e) -> p u e r", u=HALF, e=2),
-                        start=False,
-                        stop=True,
-                    )
+            nc.tensor.matmul(
+                out=sp[:],
+                lhsT=qT[b][:, n * P:(n + 1) * P],
+                rhs=kT[b][:, c * KPASS:(c + 1) * KPASS],
+                start=False,
+                stop=(i != LAST),
+            )
+            if i == LAST:
+                nc.tensor.matmul(
+                    out=sp[:].rearrange("p (u e r) -> p u e r", u=HALF, e=2),
+                    lhsT=ident_bf[:],
+                    rhs=m_sb[b][:, n, c * KPASS:(c + 1) * KPASS].rearrange("p (u r e) -> p u e r", u=HALF, e=2),
+                    start=False,
+                    stop=True,
+                )
 
-        def stage_max_last():
-            pm = small.tile([P, NPASS], F32, name="pm")
-            for c in range(NPASS):
-                nc.vector.tensor_reduce(out=pm[:, c:c + 1], in_=s_ps[(LAST, c)][:], axis=AX.X, op=ALU.max)
-            negm[LAST] = small.tile([P, 1], F32, name="negm")
-            nc.vector.tensor_reduce(out=negm[LAST][:], in_=pm[:], axis=AX.X, op=ALU.max, negate=True)
-
-        def stage_mask(i):
+        def add_mask(i, c):
             b, n = divmod(i, NT)
+            if c == 0:
+                s_sb[i] = work.tile([P, S], F32, name="s_sb")
+            nc.vector.tensor_tensor(
+                out=s_sb[i][:, c * KPASS:(c + 1) * KPASS].rearrange("p (u r e) -> p u r e", u=HALF, e=2),
+                in0=s_ps[(i, c)][:].rearrange("p (u e r) -> p u r e", u=HALF, e=2),
+                in1=m_sb[b][:, n, c * KPASS:(c + 1) * KPASS].rearrange("p (u r e) -> p u r e", u=HALF, e=2),
+                op=ALU.add,
+            )
+
+        def copy_scores(i):
             s_sb[i] = work.tile([P, S], F32, name="s_sb")
             for c in range(NPASS):
-                nc.vector.tensor_tensor(
+                nc.scalar.copy(
                     out=s_sb[i][:, c * KPASS:(c + 1) * KPASS].rearrange("p (u r e) -> p u r e", u=HALF, e=2),
-                    in0=s_ps[(i, c)][:].rearrange("p (u e r) -> p u r e", u=HALF, e=2),
-                    in1=m_sb[b][:, n, c * KPASS:(c + 1) * KPASS].rearrange("p (u r e) -> p u r e", u=HALF, e=2),
-                    op=ALU.add,
+                    in_=s_ps[(i, c)][:].rearrange("p (u e r) -> p u r e", u=HALF, e=2),
                 )
+
+        def add_mask_gpsimd(i):
+            b, n = divmod(i, NT)
+            for h in range(SPLIT):
+                cols = slice(h * S // SPLIT, (h + 1) * S // SPLIT)
+                nc.gpsimd.tensor_tensor(
+                    out=s_sb[i][:, cols], in0=s_sb[i][:, cols], in1=m_sb[b][:, n, cols], op=ALU.add
+                )
+
+        def last_max(c):
+            nc.vector.tensor_reduce(out=pm[:, c:c + 1], in_=s_ps[(LAST, c)][:], axis=AX.X, op=ALU.max)
 
         def stage_max(i):
             negm[i] = small.tile([P, 1], F32, name="negm")
-            nc.vector.tensor_reduce(out=negm[i][:], in_=s_sb[i][:], axis=AX.X, op=ALU.max, negate=True)
+            src = pm if i == LAST else s_sb[i]
+            nc.vector.tensor_reduce(out=negm[i][:], in_=src[:], axis=AX.X, op=ALU.max, negate=True)
 
         def stage_exp(i):
             e_bf[i] = work.tile([P, S], BF16, name="e_bf")
@@ -220,10 +237,11 @@ def tile_dotproductattention_kernel(tc, q, k, v, attn_mask, out):
             e_codes[i] = work.tile([P, NPASS * P], U32, name="e_codes", align_bytes=64)
             e_scl[i] = work.tile([P, NPASS * P], U8, name="e_scl", align_bytes=64)
             nc.vector.quantize_mx(out=e_codes[i][:].bitcast(FP8X4), scales=e_scl[i][:], in_=e_grp[i][:])
-            if i % 2 == 0:
-                cols = 1 if i == LAST - 1 else 2
-                rinv[i // 2] = small.tile([P, 2], F32, name="rinv")
-                nc.vector.reciprocal(out=rinv[i // 2][:, 0:cols], in_=rsum[i // 2][:, 0:cols])
+
+        def stage_reciprocal(i):
+            cols = 1 if i == LAST else 2
+            rinv[i // 2] = small.tile([P, 2], F32, name="rinv")
+            nc.vector.reciprocal(out=rinv[i // 2][:, 0:cols], in_=rsum[i // 2][:, 0:cols])
 
         def stage_pv(i):
             b = i // NT
@@ -250,49 +268,69 @@ def tile_dotproductattention_kernel(tc, q, k, v, attn_mask, out):
             elif n % 2 == 1:
                 nc.sync.dma_start(out=o_dram[b][:, n - 1:n + 1, :], in_=o_sb[b][:, n - 1:n + 1, :])
 
+        pm = const.tile([P, NPASS], F32, name="pm")
         kt0 = transpose_k(0)
         nc.vector.tensor_copy(out=kT[0][:], in_=kt0[:])
         qa = transpose_q(0, 0, 2, ps_o, "O")
         nc.scalar.copy(out=qT[0][:, 0:2 * P], in_=qa[:])
-        stage_scores(0)
+        scores(0, 0)
+        scores(0, 1)
         qb = transpose_q(0, 2, NT, ps_t, "T")
         nc.scalar.copy(out=qT[0][:, 2 * P:S], in_=qb[:])
         nc.gpsimd.tensor_scalar(
             out=v_grp[:], in0=v_sb[:].rearrange("p (g u) e d -> p g d (u e)", u=HALF),
             scalar1=1.0, scalar2=0.0, op0=ALU.mult, op1=ALU.add,
         )
-        late = {}
-        for step in range(0, NTILES):
-            if step + 1 < NTILES:
-                stage_scores(step + 1)
-            if step == 0:
-                late["k"] = transpose_k(1)
-                late["q"] = transpose_q(1, 0, NT, ps_t, "T")
-            if step == 2:
+        add_mask(0, 0)
+        scores(1, 0)
+
+        for s in range(NTILES):
+            if 2 <= s:
+                stage_group(s - 2, False)
+            if s + 3 < LAST and on_gpsimd(s + 3):
+                scores(s + 3, 0)
+                scores(s + 3, 1)
+            if s == LAST:
+                last_max(1)
+            elif not on_gpsimd(s):
+                add_mask(s, 1)
+            if s + 1 <= LAST and not on_gpsimd(s + 1):
+                scores(s + 1, 1)
+            if 3 <= s:
+                stage_quantise(s - 3)
+            if s + 3 < LAST and on_gpsimd(s + 3):
+                copy_scores(s + 3)
+            if s + 1 < LAST and on_gpsimd(s + 1):
+                add_mask_gpsimd(s + 1)
+            if s == 2:
+                kt1 = transpose_k(1)
+                nc.scalar.copy(out=kT[1][:], in_=kt1[:])
+            if s == 3:
+                qt1 = transpose_q(1, 0, NT, ps_t, "T")
+                nc.scalar.copy(out=qT[1][:], in_=qt1[:])
+            if s == 2:
                 nc.vector.quantize_mx(
                     out=v_codes[:].bitcast(FP8X4),
                     scales=v_scl[:],
                     in_=v_grp[:].rearrange("p g d t -> p (g d t)"),
                 )
-            if step != LAST:
-                stage_mask(step)
-            if 0 <= step - 3:
-                stage_quantise(step - 3)
-                stage_pv(step - 3)
-            if step == LAST:
-                stage_max_last()
-            else:
-                stage_max(step)
-            if 0 <= step - 1:
-                stage_exp(step - 1)
-                if step == 1:
-                    nc.scalar.copy(out=kT[1][:], in_=late["k"][:])
-                    nc.scalar.copy(out=qT[1][:], in_=late["q"][:])
-                stage_transpose(step - 1)
-            if 0 <= step - 2 < LAST - 2:
-                stage_group(step - 2, False)
-            if 0 <= step - 3:
-                stage_out(step - 3)
+            if 4 <= s:
+                if s % 2 == 1:
+                    stage_reciprocal(s - 4)
+                stage_pv(s - 4)
+            stage_max(s)
+            if s + 1 == LAST:
+                last_max(0)
+            elif s + 1 < LAST and not on_gpsimd(s + 1):
+                add_mask(s + 1, 0)
+            if s + 2 <= LAST and not on_gpsimd(s + 2):
+                scores(s + 2, 0)
+            if 5 <= s:
+                stage_out(s - 5)
+            if s < LAST:
+                stage_exp(s)
+            if 1 <= s:
+                stage_transpose(s - 1)
 
         b, n = divmod(LAST, NT)
         rs_h = small.tile([P, NPASS], F32, name="rs_h")
@@ -328,24 +366,28 @@ def tile_dotproductattention_kernel(tc, q, k, v, attn_mask, out):
             nc.vector.quantize_mx(out=eh_codes[c][:].bitcast(FP8X4), scales=eh_scl[c][:], in_=eh_grp[c][:])
 
         exp_half(0)
-        transpose_half(0)
-        exp_half(1)
-        transpose_half(1)
-        stage_group(LAST - 2, True)
-        stage_group(LAST - 1, True)
         stage_quantise(LAST - 2)
+        transpose_half(0)
+        stage_pv(LAST - 3)
+        exp_half(1)
+        stage_reciprocal(LAST - 2)
+        stage_out(LAST - 4)
+        transpose_half(1)
         stage_pv(LAST - 2)
-        group_half(0, False)
-        group_half(1, False)
-        stage_out(LAST - 2)
+        stage_group(LAST - 1, True)
         stage_quantise(LAST - 1)
+        group_half(0, True)
+        stage_out(LAST - 3)
+        group_half(1, False)
         stage_pv(LAST - 1)
+        stage_reciprocal(LAST)
         rs_t = small.tile([P, 1], F32, name="rs_t")
         nc.vector.tensor_reduce(out=rs_t[:], in_=rs_h[:], axis=AX.X, op=ALU.add)
         ri_t = small.tile([P, 1], F32, name="ri_t")
-        nc.vector.reciprocal(out=ri_t[:], in_=rs_t[:])
         quantise_half(0)
         quantise_half(1)
+        nc.vector.reciprocal(out=ri_t[:], in_=rs_t[:])
+        stage_out(LAST - 2)
         stage_out(LAST - 1)
         o_last = ps_o.tile([P, D], F32, tag="O", name="o_last")
         for c in range(NPASS):

@@ -37,14 +37,14 @@ SPLIT = 4
 
 
 def on_gpsimd(i):
-    return i > 1 and i % 4 == 1
+    return i > 1 and i % 3 == 1
 
 
 def tile_dotproductattention_kernel(tc, q, k, v, attn_mask, out):
     nc = tc.nc
     with ExitStack() as ctx:
         const = ctx.enter_context(tc.tile_pool(name="const", bufs=1))
-        work = ctx.enter_context(tc.tile_pool(name="work", bufs=4))
+        work = ctx.enter_context(tc.tile_pool(name="work", bufs=6))
         small = ctx.enter_context(tc.tile_pool(name="small", bufs=4))
         ps_s = ctx.enter_context(tc.psum_pool(name="ps_s", bufs=4))
         ps_t = ctx.enter_context(tc.psum_pool(name="ps_t", bufs=2))
@@ -59,6 +59,14 @@ def tile_dotproductattention_kernel(tc, q, k, v, attn_mask, out):
         m_dram = [attn_mask[b].rearrange("(p n) j -> p n j", n=NT) for b in range(BH)]
         o_dram = [out[b].rearrange("(p n) d -> p n d", n=NT) for b in range(BH)]
 
+        q_dram = [q[b].rearrange("(p n) d -> p n d", n=NT) for b in range(BH)]
+
+        def load_k(b, c):
+            nc.sync.dma_start(
+                out=k_sb[b][:, c * HALF:(c + 1) * HALF],
+                in_=k[b, c * KPASS:(c + 1) * KPASS].rearrange("(w p e) d -> p w e d", p=P, e=2),
+            )
+
         def load_kq(b):
             nc.sync.dma_start(out=k_sb[b][:], in_=k[b].rearrange("(w p e) d -> p w e d", p=P, e=2))
             nc.sync.dma_start(out=q_sb[b][:], in_=q[b].rearrange("(p n) d -> p n d", n=NT))
@@ -66,8 +74,11 @@ def tile_dotproductattention_kernel(tc, q, k, v, attn_mask, out):
         def load_mask(b, n0, n1):
             nc.sync.dma_start(out=m_sb[b][:, n0:n1, :], in_=m_dram[b][:, n0:n1, :])
 
-        load_kq(0)
+        load_k(0, 0)
+        nc.sync.dma_start(out=q_sb[0][:, 0:2, :], in_=q_dram[0][:, 0:2, :])
+        load_k(0, 1)
         load_mask(0, 0, 1)
+        nc.sync.dma_start(out=q_sb[0][:, 2:NT, :], in_=q_dram[0][:, 2:NT, :])
         load_mask(0, 1, 2)
         nc.sync.dma_start(
             out=v_sb[:],
@@ -204,6 +215,12 @@ def tile_dotproductattention_kernel(tc, q, k, v, attn_mask, out):
         def last_max(c):
             nc.vector.tensor_reduce(out=pm[:, c:c + 1], in_=s_ps[(LAST, c)][:], axis=AX.X, op=ALU.max)
 
+        def add_or_max(i, c):
+            if i == LAST:
+                last_max(c)
+            else:
+                add_mask(i, c)
+
         def stage_max(i):
             negm[i] = small.tile([P, 1], F32, name="negm")
             src = pm if i == LAST else s_sb[i]
@@ -269,10 +286,18 @@ def tile_dotproductattention_kernel(tc, q, k, v, attn_mask, out):
                 nc.sync.dma_start(out=o_dram[b][:, n - 1:n + 1, :], in_=o_sb[b][:, n - 1:n + 1, :])
 
         pm = const.tile([P, NPASS], F32, name="pm")
-        kt0 = transpose_k(0)
-        nc.vector.tensor_copy(out=kT[0][:], in_=kt0[:])
+        def transpose_k_half(c):
+            kt_ps = ps_t.tile([P, KPASS], BF16, tag="T")
+            for t in range(PACK):
+                nc.tensor.transpose(kt_ps[:, t * P:(t + 1) * P], k_sb[0][:, c * HALF + t // 2, t % 2, :], ident_bf[:])
+            return kt_ps
+
+        kt_a = transpose_k_half(0)
+        nc.vector.tensor_copy(out=kT[0][:, 0:KPASS], in_=kt_a[:])
         qa = transpose_q(0, 0, 2, ps_o, "O")
         nc.scalar.copy(out=qT[0][:, 0:2 * P], in_=qa[:])
+        kt_b = transpose_k_half(1)
+        nc.scalar.copy(out=kT[0][:, KPASS:S], in_=kt_b[:])
         scores(0, 0)
         scores(0, 1)
         qb = transpose_q(0, 2, NT, ps_t, "T")
@@ -282,53 +307,47 @@ def tile_dotproductattention_kernel(tc, q, k, v, attn_mask, out):
             scalar1=1.0, scalar2=0.0, op0=ALU.mult, op1=ALU.add,
         )
         add_mask(0, 0)
-        scores(1, 0)
+        add_mask(0, 1)
 
-        for s in range(NTILES):
-            if 2 <= s:
-                stage_group(s - 2, False)
-            if s + 3 < LAST and on_gpsimd(s + 3):
-                scores(s + 3, 0)
-                scores(s + 3, 1)
-            if s == LAST:
-                last_max(1)
-            elif not on_gpsimd(s):
-                add_mask(s, 1)
-            if s + 1 <= LAST and not on_gpsimd(s + 1):
-                scores(s + 1, 1)
-            if 3 <= s:
-                stage_quantise(s - 3)
-            if s + 3 < LAST and on_gpsimd(s + 3):
-                copy_scores(s + 3)
-            if s + 1 < LAST and on_gpsimd(s + 1):
-                add_mask_gpsimd(s + 1)
+        for s in range(LAST):
+            if 1 <= s:
+                stage_exp(s - 1)
             if s == 2:
-                kt1 = transpose_k(1)
-                nc.scalar.copy(out=kT[1][:], in_=kt1[:])
-            if s == 3:
                 qt1 = transpose_q(1, 0, NT, ps_t, "T")
                 nc.scalar.copy(out=qT[1][:], in_=qt1[:])
-            if s == 2:
                 nc.vector.quantize_mx(
                     out=v_codes[:].bitcast(FP8X4),
                     scales=v_scl[:],
                     in_=v_grp[:].rearrange("p g d t -> p (g d t)"),
                 )
-            if 4 <= s:
-                if s % 2 == 1:
-                    stage_reciprocal(s - 4)
-                stage_pv(s - 4)
+            if 2 <= s:
+                stage_group(s - 2, False)
+            if not on_gpsimd(s + 1):
+                scores(s + 1, 0)
+            if 3 <= s:
+                stage_quantise(s - 3)
             stage_max(s)
-            if s + 1 == LAST:
-                last_max(0)
-            elif s + 1 < LAST and not on_gpsimd(s + 1):
-                add_mask(s + 1, 0)
-            if s + 2 <= LAST and not on_gpsimd(s + 2):
-                scores(s + 2, 0)
             if 5 <= s:
                 stage_out(s - 5)
-            if s < LAST:
-                stage_exp(s)
+            if s == 3:
+                kt1 = transpose_k(1)
+                nc.scalar.copy(out=kT[1][:], in_=kt1[:])
+            if 3 <= s and s % 2 == 1:
+                stage_reciprocal(s - 2)
+            if s + 3 < LAST and on_gpsimd(s + 3):
+                copy_scores(s + 3)
+            if on_gpsimd(s + 1):
+                add_mask_gpsimd(s + 1)
+            else:
+                scores(s + 1, 1)
+                add_or_max(s + 1, 0)
+            if 4 <= s:
+                stage_pv(s - 4)
+            if s + 4 < LAST and on_gpsimd(s + 4):
+                scores(s + 4, 0)
+                scores(s + 4, 1)
+            if not on_gpsimd(s + 1):
+                add_or_max(s + 1, 1)
             if 1 <= s:
                 stage_transpose(s - 1)
 
@@ -365,30 +384,36 @@ def tile_dotproductattention_kernel(tc, q, k, v, attn_mask, out):
             eh_scl[c] = work.tile([P, P], U8, name="eh_scl", align_bytes=64)
             nc.vector.quantize_mx(out=eh_codes[c][:].bitcast(FP8X4), scales=eh_scl[c][:], in_=eh_grp[c][:])
 
+        stage_exp(LAST - 1)
+        stage_quantise(LAST - 3)
+        stage_pv(LAST - 4)
+        stage_max(LAST)
+        stage_group(LAST - 2, True)
+        stage_transpose(LAST - 1)
         exp_half(0)
-        stage_quantise(LAST - 2)
         transpose_half(0)
-        stage_pv(LAST - 3)
         exp_half(1)
-        stage_reciprocal(LAST - 2)
-        stage_out(LAST - 4)
         transpose_half(1)
-        stage_pv(LAST - 2)
         stage_group(LAST - 1, True)
-        stage_quantise(LAST - 1)
+        stage_out(LAST - 5)
+        stage_pv(LAST - 3)
+        stage_quantise(LAST - 2)
+        stage_out(LAST - 4)
+        stage_pv(LAST - 2)
         group_half(0, True)
-        stage_out(LAST - 3)
         group_half(1, False)
+        stage_reciprocal(LAST - 2)
+        stage_quantise(LAST - 1)
+        stage_out(LAST - 3)
         stage_pv(LAST - 1)
-        stage_reciprocal(LAST)
         rs_t = small.tile([P, 1], F32, name="rs_t")
         nc.vector.tensor_reduce(out=rs_t[:], in_=rs_h[:], axis=AX.X, op=ALU.add)
-        ri_t = small.tile([P, 1], F32, name="ri_t")
         quantise_half(0)
         quantise_half(1)
+        stage_reciprocal(LAST)
+        ri_t = small.tile([P, 1], F32, name="ri_t")
         nc.vector.reciprocal(out=ri_t[:], in_=rs_t[:])
         stage_out(LAST - 2)
-        stage_out(LAST - 1)
         o_last = ps_o.tile([P, D], F32, tag="O", name="o_last")
         for c in range(NPASS):
             g = b * NPASS + c
@@ -401,5 +426,6 @@ def tile_dotproductattention_kernel(tc, q, k, v, attn_mask, out):
                 start=(c == 0),
                 stop=(c == NPASS - 1),
             )
+        stage_out(LAST - 1)
         nc.scalar.activation(out=o_sb[b][:, n, :], in_=o_last[:], func=ACT.Copy, scale=ri_t[:])
         nc.sync.dma_start(out=o_dram[b][:, n:n + 1, :], in_=o_sb[b][:, n:n + 1, :])

@@ -17,6 +17,8 @@ AX = mybir.AxisListType
 P = 128
 BH, S, D = 2, 1024, 128
 NT = S // P
+NTILES = BH * NT
+LAST = NTILES - 1
 PACK = 4
 KPASS = P * PACK
 NPASS = S // KPASS
@@ -31,13 +33,15 @@ C_HI = round(LN_A * 2.0 ** 20) / 2.0 ** 20
 C_LO = LN_A - C_HI
 
 FLOPS = 2 * 2 * BH * S * S * D
-WARM = 5
-WARM_N = 256
-SPLIT = 4
+WARM = 12
+WARM_N = 128
+QUARTER = KPASS // 2
 
 
-def on_gpsimd(i):
-    return i > 1 and i % 3 == 1
+def pieces_on_gpsimd(i):
+    if i < 2 or i == LAST:
+        return 0
+    return 2 if i % 3 == 2 else 1
 
 
 def tile_dotproductattention_kernel(tc, q, k, v, attn_mask, out):
@@ -152,8 +156,6 @@ def tile_dotproductattention_kernel(tc, q, k, v, attn_mask, out):
                 nc.tensor.transpose(qt_ps[:, (n - n0) * P:(n - n0 + 1) * P], q_sb[b][:, n, :], ident_bf[:])
             return qt_ps
 
-        NTILES = BH * NT
-        LAST = NTILES - 1
         s_ps, s_sb, negm, e_bf, rsum, rinv, e_ps, e_grp, e_codes, e_scl, o_ps = {}, {}, {}, {}, {}, {}, {}, {}, {}, {}, {}
 
         def scores(i, c):
@@ -185,31 +187,42 @@ def tile_dotproductattention_kernel(tc, q, k, v, attn_mask, out):
                     stop=True,
                 )
 
+        def natural(ap, n):
+            return ap.rearrange("p (w e r) -> p w r e", w=n, e=2)
+
+        def paired(ap, n):
+            return ap.rearrange("p (w r e) -> p w r e", w=n, e=2)
+
+        def new_scores(i):
+            if i not in s_sb:
+                s_sb[i] = work.tile([P, S], F32, name="s_sb")
+
         def add_mask(i, c):
             b, n = divmod(i, NT)
-            if c == 0:
-                s_sb[i] = work.tile([P, S], F32, name="s_sb")
+            new_scores(i)
+            left = HALF - pieces_on_gpsimd(i) if c == 0 else HALF
+            if left == 0:
+                return
+            keys = slice(c * KPASS, c * KPASS + left * QUARTER)
             nc.vector.tensor_tensor(
-                out=s_sb[i][:, c * KPASS:(c + 1) * KPASS].rearrange("p (u r e) -> p u r e", u=HALF, e=2),
-                in0=s_ps[(i, c)][:].rearrange("p (u e r) -> p u r e", u=HALF, e=2),
-                in1=m_sb[b][:, n, c * KPASS:(c + 1) * KPASS].rearrange("p (u r e) -> p u r e", u=HALF, e=2),
+                out=paired(s_sb[i][:, keys], left),
+                in0=natural(s_ps[(i, c)][:, 0:left * QUARTER], left),
+                in1=paired(m_sb[b][:, n, keys], left),
                 op=ALU.add,
             )
 
         def copy_scores(i):
-            s_sb[i] = work.tile([P, S], F32, name="s_sb")
-            for c in range(NPASS):
-                nc.scalar.copy(
-                    out=s_sb[i][:, c * KPASS:(c + 1) * KPASS].rearrange("p (u r e) -> p u r e", u=HALF, e=2),
-                    in_=s_ps[(i, c)][:].rearrange("p (u e r) -> p u r e", u=HALF, e=2),
-                )
+            new_scores(i)
+            k_ = pieces_on_gpsimd(i)
+            cols = slice(KPASS - k_ * QUARTER, KPASS)
+            nc.scalar.copy(out=paired(s_sb[i][:, cols], k_), in_=natural(s_ps[(i, 0)][:, cols], k_))
 
         def add_mask_gpsimd(i):
             b, n = divmod(i, NT)
-            for h in range(SPLIT):
-                cols = slice(h * S // SPLIT, (h + 1) * S // SPLIT)
+            for h in range(HALF - pieces_on_gpsimd(i), HALF):
+                keys = slice(h * QUARTER, (h + 1) * QUARTER)
                 nc.gpsimd.tensor_tensor(
-                    out=s_sb[i][:, cols], in0=s_sb[i][:, cols], in1=m_sb[b][:, n, cols], op=ALU.add
+                    out=s_sb[i][:, keys], in0=s_sb[i][:, keys], in1=m_sb[b][:, n, keys], op=ALU.add
                 )
 
         def last_max(c):
@@ -307,49 +320,51 @@ def tile_dotproductattention_kernel(tc, q, k, v, attn_mask, out):
             scalar1=1.0, scalar2=0.0, op0=ALU.mult, op1=ALU.add,
         )
         add_mask(0, 0)
+        scores(1, 0)
         add_mask(0, 1)
+        scores(1, 1)
+        scores(2, 0)
+        stage_max(0)
+        add_mask(1, 1)
 
-        for s in range(LAST):
+        for s in range(LAST - 1):
             if 1 <= s:
                 stage_exp(s - 1)
-            if s == 2:
+            if 4 <= s:
+                stage_quantise(s - 4)
+            if 2 <= s:
+                stage_transpose(s - 2)
+            if 5 <= s:
+                stage_out(s - 5)
+            if 2 <= s:
+                stage_group(s - 2, False)
+            if 1 <= s:
+                add_mask_gpsimd(s + 1)
+            add_mask(s + 1, 0)
+            if s + 2 < LAST:
+                copy_scores(s + 2)
+            if s == 0:
+                kt1 = transpose_k(1)
+                nc.scalar.copy(out=kT[1][:], in_=kt1[:])
+            if s == 3:
                 qt1 = transpose_q(1, 0, NT, ps_t, "T")
                 nc.scalar.copy(out=qT[1][:], in_=qt1[:])
+            scores(s + 2, 1)
+            if s + 3 <= LAST:
+                scores(s + 3, 0)
+            if s == 3:
                 nc.vector.quantize_mx(
                     out=v_codes[:].bitcast(FP8X4),
                     scales=v_scl[:],
                     in_=v_grp[:].rearrange("p g d t -> p (g d t)"),
                 )
-            if 2 <= s:
-                stage_group(s - 2, False)
-            if not on_gpsimd(s + 1):
-                scores(s + 1, 0)
-            if 3 <= s:
-                stage_quantise(s - 3)
-            stage_max(s)
-            if 5 <= s:
-                stage_out(s - 5)
-            if s == 3:
-                kt1 = transpose_k(1)
-                nc.scalar.copy(out=kT[1][:], in_=kt1[:])
-            if 3 <= s and s % 2 == 1:
-                stage_reciprocal(s - 2)
-            if s + 3 < LAST and on_gpsimd(s + 3):
-                copy_scores(s + 3)
-            if on_gpsimd(s + 1):
-                add_mask_gpsimd(s + 1)
-            else:
-                scores(s + 1, 1)
-                add_or_max(s + 1, 0)
             if 4 <= s:
                 stage_pv(s - 4)
-            if s + 4 < LAST and on_gpsimd(s + 4):
-                scores(s + 4, 0)
-                scores(s + 4, 1)
-            if not on_gpsimd(s + 1):
-                add_or_max(s + 1, 1)
+            if 3 <= s and s % 2 == 1:
+                stage_reciprocal(s - 2)
             if 1 <= s:
-                stage_transpose(s - 1)
+                stage_max(s)
+            add_or_max(s + 2, 1)
 
         b, n = divmod(LAST, NT)
         rs_h = small.tile([P, NPASS], F32, name="rs_h")
@@ -384,16 +399,26 @@ def tile_dotproductattention_kernel(tc, q, k, v, attn_mask, out):
             eh_scl[c] = work.tile([P, P], U8, name="eh_scl", align_bytes=64)
             nc.vector.quantize_mx(out=eh_codes[c][:].bitcast(FP8X4), scales=eh_scl[c][:], in_=eh_grp[c][:])
 
-        stage_exp(LAST - 1)
-        stage_quantise(LAST - 3)
-        stage_pv(LAST - 4)
+        stage_exp(LAST - 2)
+        stage_max(LAST - 1)
+        stage_transpose(LAST - 3)
+        stage_out(LAST - 6)
+        stage_group(LAST - 3, False)
+        last_max(0)
+        stage_quantise(LAST - 5)
         stage_max(LAST)
+        stage_transpose(LAST - 2)
+        stage_exp(LAST - 1)
+        stage_pv(LAST - 5)
+        stage_quantise(LAST - 4)
+        stage_pv(LAST - 4)
         stage_group(LAST - 2, True)
         stage_transpose(LAST - 1)
         exp_half(0)
         transpose_half(0)
         exp_half(1)
         transpose_half(1)
+        stage_quantise(LAST - 3)
         stage_group(LAST - 1, True)
         stage_out(LAST - 5)
         stage_pv(LAST - 3)

@@ -84,13 +84,15 @@ def tile_dotproductattention_kernel(tc, q, k, v, attn_mask, out):
         load_mask(0, 0, 1)
         nc.sync.dma_start(out=q_sb[0][:, 2:NT, :], in_=q_dram[0][:, 2:NT, :])
         load_mask(0, 1, 2)
+        load_mask(0, 2, 3)
         nc.sync.dma_start(
             out=v_sb[:],
             in_=v.flatten_outer_dims().rearrange("(w p e) d -> p w e d", p=P, e=2),
         )
+        load_mask(0, 3, 4)
+        load_mask(0, 4, 6)
         load_kq(1)
-        load_mask(0, 2, 4)
-        load_mask(0, 4, 8)
+        load_mask(0, 6, 8)
         load_mask(1, 0, 4)
         load_mask(1, 4, 8)
 
@@ -343,7 +345,7 @@ def tile_dotproductattention_kernel(tc, q, k, v, attn_mask, out):
             add_mask(s + 1, 0)
             if s + 2 < LAST:
                 copy_scores(s + 2)
-            if s == 0:
+            if s == 2:
                 kt1 = transpose_k(1)
                 nc.scalar.copy(out=kT[1][:], in_=kt1[:])
             if s == 3:

import math
from contextlib import ExitStack

import concourse.mybir as mybir
from concourse.masks import make_identity

F32 = mybir.dt.float32
BF16 = mybir.dt.bfloat16
I32 = mybir.dt.int32
U32 = mybir.dt.uint32
U8 = mybir.dt.uint8
FP8X4 = mybir.dt.float8_e4m3fn_x4
ALU = mybir.AluOpType
ACT = mybir.ActivationFunctionType
AX = mybir.AxisListType

P = 128
BH, S, D = 2, 1024, 128
NT = S // P
NTILES = BH * NT
LAST = NTILES - 1
PACK = 4
KPASS = P * PACK
NPASS = S // KPASS
NBLK = NPASS * PACK
HALF = 2
NWORD = NPASS * HALF

ALPHA = 0.99
EPS = 1e-10
LN_A = math.log(ALPHA)
C_HI = round(LN_A * 2.0 ** 20) / 2.0 ** 20
C_LO = LN_A - C_HI

FLOPS = 2 * 2 * BH * S * S * D
WARM = 12
WARM_N = 128
QUARTER = KPASS // 2


def pieces_on_gpsimd(i):
    if i < 2 or i == LAST:
        return 0
    return 2 if i % 3 == 2 else 1


def tile_dotproductattention_kernel(tc, q, k, v, attn_mask, out):
    nc = tc.nc
    with ExitStack() as ctx:
        const = ctx.enter_context(tc.tile_pool(name="const", bufs=1))
        work = ctx.enter_context(tc.tile_pool(name="work", bufs=6))
        small = ctx.enter_context(tc.tile_pool(name="small", bufs=4))
        ps_s = ctx.enter_context(tc.psum_pool(name="ps_s", bufs=4))
        ps_t = ctx.enter_context(tc.psum_pool(name="ps_t", bufs=2))
        ps_o = ctx.enter_context(tc.psum_pool(name="ps_o", bufs=2))

        ctx.enter_context(tc.manual_schedule())

        k_sb = [const.tile([P, NPASS * HALF, 2, D], BF16, name="k_sb%d" % b) for b in range(BH)]
        q_sb = [const.tile([P, NT, D], BF16, name="q_sb%d" % b) for b in range(BH)]
        m_sb = [const.tile([P, NT, S], BF16, name="m_sb%d" % b) for b in range(BH)]
        v_sb = const.tile([P, BH * NWORD, 2, D], BF16, name="v_sb")
        m_dram = [attn_mask[b].rearrange("(p n) j -> p n j", n=NT) for b in range(BH)]
        o_dram = [out[b].rearrange("(p n) d -> p n d", n=NT) for b in range(BH)]

        q_dram = [q[b].rearrange("(p n) d -> p n d", n=NT) for b in range(BH)]

        def load_k(b, c):
            nc.sync.dma_start(
                out=k_sb[b][:, c * HALF:(c + 1) * HALF],
                in_=k[b, c * KPASS:(c + 1) * KPASS].rearrange("(w p e) d -> p w e d", p=P, e=2),
            )

        def load_kq(b):
            nc.sync.dma_start(out=k_sb[b][:], in_=k[b].rearrange("(w p e) d -> p w e d", p=P, e=2))
            nc.sync.dma_start(out=q_sb[b][:], in_=q[b].rearrange("(p n) d -> p n d", n=NT))

        def load_mask(b, n0, n1):
            nc.sync.dma_start(out=m_sb[b][:, n0:n1, :], in_=m_dram[b][:, n0:n1, :])

        load_k(0, 0)
        nc.sync.dma_start(out=q_sb[0][:, 0:2, :], in_=q_dram[0][:, 0:2, :])
        load_k(0, 1)
        load_mask(0, 0, 1)
        nc.sync.dma_start(out=q_sb[0][:, 2:NT, :], in_=q_dram[0][:, 2:NT, :])
        load_mask(0, 1, 2)
        load_mask(0, 2, 3)
        nc.sync.dma_start(
            out=v_sb[:],
            in_=v.flatten_outer_dims().rearrange("(w p e) d -> p w e d", p=P, e=2),
        )
        load_mask(0, 3, 4)
        load_mask(0, 4, 6)
        load_kq(1)
        load_mask(0, 6, 8)
        load_mask(1, 0, 4)
        load_mask(1, 4, 8)

        warm_in = const.tile([P, PACK * WARM_N], BF16, name="warm_in", align_bytes=64)
        nc.vector.memset(warm_in[:].bitcast(I32), 0)
        warm_w = const.tile([P, WARM_N], U32, name="warm_w", align_bytes=64)
        warm_s = const.tile([P, WARM_N], U8, name="warm_s", align_bytes=64)

        n_i = const.tile([P, NBLK], I32, name="n_i")
        nc.gpsimd.iota(n_i[:], pattern=[[-2 * P, NWORD], [-1, 2]], base=S - 1, channel_multiplier=-2)
        ident_bf = const.tile([P, P], BF16, name="ident_bf")
        make_identity(nc, ident_bf[:])
        ident_f = const.tile([P, P], F32, name="ident_f")
        make_identity(nc, ident_f[:])

        n_f = const.tile([P, NBLK], F32, name="n_f")
        nc.vector.tensor_copy(out=n_f[:], in_=n_i[:])
        nc.vector.quantize_mx(out=warm_w[:].bitcast(FP8X4), scales=warm_s[:], in_=warm_in[:])
        warm_ps = ps_s.tile([P, WARM_N], F32, tag="S", name="warm_ps")
        for r in range(WARM):
            nc.tensor.matmul_mx(
                out=warm_ps[:],
                lhsT=warm_w[:, 0:P].bitcast(FP8X4),
                lhsT_scale=warm_s[:, 0:P],
                rhs=warm_w[:].bitcast(FP8X4),
                rhs_scale=warm_s[:],
                start=True,
                stop=True,
            )
        y = const.tile([P, NBLK], F32, name="y")
        nc.scalar.activation(out=y[:], in_=n_f[:], func=ACT.Exp, scale=-LN_A)
        w = const.tile([P, NBLK], F32, name="w")
        nc.vector.tensor_scalar(out=w[:], in0=y[:], scalar1=-0.5 * EPS, scalar2=1.0, op0=ALU.mult, op1=ALU.add)
        dl = const.tile([P, NBLK], F32, name="dl")
        nc.vector.scalar_tensor_tensor(out=dl[:], in0=y[:], scalar=EPS, in1=w[:], op0=ALU.mult, op1=ALU.mult)
        lo = const.tile([P, NBLK], F32, name="lo")
        nc.vector.scalar_tensor_tensor(out=lo[:], in0=n_f[:], scalar=C_LO, in1=dl[:], op0=ALU.mult, op1=ALU.add)
        ld = const.tile([P, NBLK], F32, name="ld")
        nc.vector.scalar_tensor_tensor(out=ld[:], in0=n_f[:], scalar=C_HI, in1=lo[:], op0=ALU.mult, op1=ALU.add)
        ld_rep = const.tile([P, NBLK, P], F32, name="ld_rep")
        for c in range(NPASS):
            blk = slice(c * PACK, (c + 1) * PACK)
            nc.vector.tensor_copy(out=ld_rep[:, blk, :], in_=ld[:, blk].unsqueeze(2).to_broadcast([P, PACK, P]))

        kT = [const.tile([P, S], BF16, name="kT%d" % b) for b in range(BH)]
        qT = [const.tile([P, S], BF16, name="qT%d" % b) for b in range(BH)]
        v_grp = const.tile([P, BH * NPASS, D, PACK], BF16, name="v_grp", align_bytes=64)
        v_codes = const.tile([P, BH * NPASS * D], U32, name="v_codes", align_bytes=64)
        v_scl = const.tile([P, BH * NPASS * D], U8, name="v_scl", align_bytes=64)
        o_sb = [const.tile([P, NT, D], F32, name="o_sb%d" % b) for b in range(BH)]

        def transpose_k(b):
            kt_ps = ps_t.tile([P, S], BF16, tag="T")
            for w_ in range(NWORD):
                for e in range(2):
                    g = 2 * w_ + e
                    nc.tensor.transpose(kt_ps[:, g * P:(g + 1) * P], k_sb[b][:, w_, e, :], ident_bf[:])
            return kt_ps

        def transpose_q(b, n0, n1, pool, tag):
            qt_ps = pool.tile([P, (n1 - n0) * P], BF16, tag=tag)
            for n in range(n0, n1):
                nc.tensor.transpose(qt_ps[:, (n - n0) * P:(n - n0 + 1) * P], q_sb[b][:, n, :], ident_bf[:])
            return qt_ps

        s_ps, s_sb, negm, e_bf, rsum, rinv, e_ps, e_grp, e_codes, e_scl, o_ps = {}, {}, {}, {}, {}, {}, {}, {}, {}, {}, {}

        def scores(i, c):
            b, n = divmod(i, NT)
            sp = ps_s.tile([P, KPASS], F32, tag="S", name="s_ps")
            s_ps[(i, c)] = sp
            for t in range(PACK):
                nc.tensor.matmul(
                    out=sp[:, t * P:(t + 1) * P],
                    lhsT=ld_rep[:, c * PACK + t, :],
                    rhs=ident_f[:],
                    is_transpose=True,
                    start=(t == 0),
                    stop=False,
                )
            nc.tensor.matmul(
                out=sp[:],
                lhsT=qT[b][:, n * P:(n + 1) * P],
                rhs=kT[b][:, c * KPASS:(c + 1) * KPASS],
                start=False,
                stop=(i != LAST),
            )
            if i == LAST:
                nc.tensor.matmul(
                    out=sp[:].rearrange("p (u e r) -> p u e r", u=HALF, e=2),
                    lhsT=ident_bf[:],
                    rhs=m_sb[b][:, n, c * KPASS:(c + 1) * KPASS].rearrange("p (u r e) -> p u e r", u=HALF, e=2),
                    start=False,
                    stop=True,
                )

        def natural(ap, n):
            return ap.rearrange("p (w e r) -> p w r e", w=n, e=2)

        def paired(ap, n):
            return ap.rearrange("p (w r e) -> p w r e", w=n, e=2)

        def new_scores(i):
            if i not in s_sb:
                s_sb[i] = work.tile([P, S], F32, name="s_sb")

        def add_mask(i, c):
            b, n = divmod(i, NT)
            new_scores(i)
            left = HALF - pieces_on_gpsimd(i) if c == 0 else HALF
            if left == 0:
                return
            keys = slice(c * KPASS, c * KPASS + left * QUARTER)
            nc.vector.tensor_tensor(
                out=paired(s_sb[i][:, keys], left),
                in0=natural(s_ps[(i, c)][:, 0:left * QUARTER], left),
                in1=paired(m_sb[b][:, n, keys], left),
                op=ALU.add,
            )

        def copy_scores(i):
            new_scores(i)
            k_ = pieces_on_gpsimd(i)
            cols = slice(KPASS - k_ * QUARTER, KPASS)
            nc.scalar.copy(out=paired(s_sb[i][:, cols], k_), in_=natural(s_ps[(i, 0)][:, cols], k_))

        def add_mask_gpsimd(i):
            b, n = divmod(i, NT)
            for h in range(HALF - pieces_on_gpsimd(i), HALF):
                keys = slice(h * QUARTER, (h + 1) * QUARTER)
                nc.gpsimd.tensor_tensor(
                    out=s_sb[i][:, keys], in0=s_sb[i][:, keys], in1=m_sb[b][:, n, keys], op=ALU.add
                )

        def last_max(c):
            nc.vector.tensor_reduce(out=pm[:, c:c + 1], in_=s_ps[(LAST, c)][:], axis=AX.X, op=ALU.max)

        def add_or_max(i, c):
            if i == LAST:
                last_max(c)
            else:
                add_mask(i, c)

        def stage_max(i):
            negm[i] = small.tile([P, 1], F32, name="negm")
            src = pm if i == LAST else s_sb[i]
            nc.vector.tensor_reduce(out=negm[i][:], in_=src[:], axis=AX.X, op=ALU.max, negate=True)

        def stage_exp(i):
            e_bf[i] = work.tile([P, S], BF16, name="e_bf")
            if i % 2 == 0:
                rsum[i // 2] = small.tile([P, 2], F32, name="rsum")
            nc.scalar.activation(
                out=e_bf[i][:], in_=s_sb[i][:], func=ACT.Exp, bias=negm[i][:], scale=1.0,
                accum_out=rsum[i // 2][:, i % 2:i % 2 + 1],
            )

        def stage_transpose(i):
            e_ps[i] = ps_t.tile([P, NWORD * P], F32, tag="T", name="e_ps")
            words = e_bf[i][:].bitcast(F32)
            for g in range(NWORD):
                nc.tensor.transpose(e_ps[i][:, g * P:(g + 1) * P], words[:, g * P:(g + 1) * P], ident_f[:])

        def stage_group(i, on_vector):
            e_grp[i] = work.tile([P, S], BF16, name="e_grp", align_bytes=64)
            dst = e_grp[i][:].bitcast(F32).rearrange("p (c i u) -> p c i u", c=NPASS, u=HALF)
            src = e_ps[i][:].rearrange("p (c u i) -> p c i u", c=NPASS, u=HALF)
            if on_vector:
                nc.vector.tensor_copy(out=dst, in_=src)
            else:
                nc.scalar.copy(out=dst, in_=src)

        def stage_quantise(i):
            e_codes[i] = work.tile([P, NPASS * P], U32, name="e_codes", align_bytes=64)
            e_scl[i] = work.tile([P, NPASS * P], U8, name="e_scl", align_bytes=64)
            nc.vector.quantize_mx(out=e_codes[i][:].bitcast(FP8X4), scales=e_scl[i][:], in_=e_grp[i][:])

        def stage_reciprocal(i):
            cols = 1 if i == LAST else 2
            rinv[i // 2] = small.tile([P, 2], F32, name="rinv")
            nc.vector.reciprocal(out=rinv[i // 2][:, 0:cols], in_=rsum[i // 2][:, 0:cols])

        def stage_pv(i):
            b = i // NT
            o_ps[i] = ps_o.tile([P, D], F32, tag="O", name="o_ps")
            for c in range(NPASS):
                g = b * NPASS + c
                nc.tensor.matmul_mx(
                    out=o_ps[i][:],
                    lhsT=e_codes[i][:, c * P:(c + 1) * P].bitcast(FP8X4),
                    lhsT_scale=e_scl[i][:, c * P:(c + 1) * P],
                    rhs=v_codes[:, g * D:(g + 1) * D].bitcast(FP8X4),
                    rhs_scale=v_scl[:, g * D:(g + 1) * D],
                    start=(c == 0),
                    stop=(c == NPASS - 1),
                )

        def stage_out(i):
            b, n = divmod(i, NT)
            nc.scalar.activation(
                out=o_sb[b][:, n, :], in_=o_ps[i][:], func=ACT.Copy, scale=rinv[i // 2][:, i % 2:i % 2 + 1]
            )
            if i == LAST - 1:
                nc.sync.dma_start(out=o_dram[b][:, n:n + 1, :], in_=o_sb[b][:, n:n + 1, :])
            elif n % 2 == 1:
                nc.sync.dma_start(out=o_dram[b][:, n - 1:n + 1, :], in_=o_sb[b][:, n - 1:n + 1, :])

        pm = const.tile([P, NPASS], F32, name="pm")
        def transpose_k_half(c):
            kt_ps = ps_t.tile([P, KPASS], BF16, tag="T")
            for t in range(PACK):
                nc.tensor.transpose(kt_ps[:, t * P:(t + 1) * P], k_sb[0][:, c * HALF + t // 2, t % 2, :], ident_bf[:])
            return kt_ps

        kt_a = transpose_k_half(0)
        nc.vector.tensor_copy(out=kT[0][:, 0:KPASS], in_=kt_a[:])
        qa = transpose_q(0, 0, 2, ps_o, "O")
        nc.scalar.copy(out=qT[0][:, 0:2 * P], in_=qa[:])
        kt_b = transpose_k_half(1)
        nc.scalar.copy(out=kT[0][:, KPASS:S], in_=kt_b[:])
        scores(0, 0)
        scores(0, 1)
        qb = transpose_q(0, 2, NT, ps_t, "T")
        nc.scalar.copy(out=qT[0][:, 2 * P:S], in_=qb[:])
        nc.gpsimd.tensor_scalar(
            out=v_grp[:], in0=v_sb[:].rearrange("p (g u) e d -> p g d (u e)", u=HALF),
            scalar1=1.0, scalar2=0.0, op0=ALU.mult, op1=ALU.add,
        )
        add_mask(0, 0)
        scores(1, 0)
        add_mask(0, 1)
        scores(1, 1)
        scores(2, 0)
        stage_max(0)
        add_mask(1, 1)

        for s in range(LAST - 1):
            if 1 <= s:
                stage_exp(s - 1)
            if 4 <= s:
                stage_quantise(s - 4)
            if 2 <= s:
                stage_transpose(s - 2)
            if 5 <= s:
                stage_out(s - 5)
            if 2 <= s:
                stage_group(s - 2, False)
            if 1 <= s:
                add_mask_gpsimd(s + 1)
            add_mask(s + 1, 0)
            if s + 2 < LAST:
                copy_scores(s + 2)
            if s == 2:
                kt1 = transpose_k(1)
                nc.scalar.copy(out=kT[1][:], in_=kt1[:])
            if s == 3:
                qt1 = transpose_q(1, 0, NT, ps_t, "T")
                nc.scalar.copy(out=qT[1][:], in_=qt1[:])
            scores(s + 2, 1)
            if s + 3 <= LAST:
                scores(s + 3, 0)
            if s == 3:
                nc.vector.quantize_mx(
                    out=v_codes[:].bitcast(FP8X4),
                    scales=v_scl[:],
                    in_=v_grp[:].rearrange("p g d t -> p (g d t)"),
                )
            if 4 <= s:
                stage_pv(s - 4)
            if 3 <= s and s % 2 == 1:
                stage_reciprocal(s - 2)
            if 1 <= s:
                stage_max(s)
            add_or_max(s + 2, 1)

        b, n = divmod(LAST, NT)
        rs_h = small.tile([P, NPASS], F32, name="rs_h")
        eh_bf, eh_ps, eh_grp, eh_codes, eh_scl = {}, {}, {}, {}, {}

        def exp_half(c):
            eh_bf[c] = work.tile([P, KPASS], BF16, name="eh_bf")
            nc.scalar.activation(
                out=eh_bf[c][:].rearrange("p (u r e) -> p u r e", u=HALF, e=2),
                in_=s_ps[(LAST, c)][:].rearrange("p (u e r) -> p u r e", u=HALF, e=2),
                func=ACT.Exp, bias=negm[LAST][:], scale=1.0,
                accum_out=rs_h[:, c:c + 1],
            )

        def transpose_half(c):
            eh_ps[c] = ps_s.tile([P, HALF * P], F32, tag="S", name="eh_ps")
            words = eh_bf[c][:].bitcast(F32)
            for u in range(HALF):
                nc.tensor.transpose(eh_ps[c][:, u * P:(u + 1) * P], words[:, u * P:(u + 1) * P], ident_f[:])

        def group_half(c, on_vector):
            eh_grp[c] = work.tile([P, KPASS], BF16, name="eh_grp", align_bytes=64)
            dst = eh_grp[c][:].bitcast(F32).rearrange("p (i u) -> p i u", u=HALF)
            src = eh_ps[c][:].rearrange("p (u i) -> p i u", u=HALF)
            if on_vector:
                nc.vector.tensor_copy(out=dst, in_=src)
            else:
                nc.scalar.copy(out=dst, in_=src)

        def quantise_half(c):
            eh_codes[c] = work.tile([P, P], U32, name="eh_codes", align_bytes=64)
            eh_scl[c] = work.tile([P, P], U8, name="eh_scl", align_bytes=64)
            nc.vector.quantize_mx(out=eh_codes[c][:].bitcast(FP8X4), scales=eh_scl[c][:], in_=eh_grp[c][:])

        stage_exp(LAST - 2)
        stage_max(LAST - 1)
        stage_transpose(LAST - 3)
        stage_out(LAST - 6)
        stage_group(LAST - 3, False)
        last_max(0)
        stage_quantise(LAST - 5)
        stage_max(LAST)
        stage_transpose(LAST - 2)
        stage_exp(LAST - 1)
        stage_pv(LAST - 5)
        stage_quantise(LAST - 4)
        stage_pv(LAST - 4)
        stage_group(LAST - 2, True)
        stage_transpose(LAST - 1)
        exp_half(0)
        transpose_half(0)
        exp_half(1)
        transpose_half(1)
        stage_quantise(LAST - 3)
        stage_group(LAST - 1, True)
        stage_out(LAST - 5)
        stage_pv(LAST - 3)
        stage_quantise(LAST - 2)
        stage_out(LAST - 4)
        stage_pv(LAST - 2)
        group_half(0, True)
        group_half(1, False)
        stage_reciprocal(LAST - 2)
        stage_quantise(LAST - 1)
        stage_out(LAST - 3)
        stage_pv(LAST - 1)
        rs_t = small.tile([P, 1], F32, name="rs_t")
        nc.vector.tensor_reduce(out=rs_t[:], in_=rs_h[:], axis=AX.X, op=ALU.add)
        quantise_half(0)
        quantise_half(1)
        stage_reciprocal(LAST)
        ri_t = small.tile([P, 1], F32, name="ri_t")
        nc.vector.reciprocal(out=ri_t[:], in_=rs_t[:])
        stage_out(LAST - 2)
        o_last = ps_o.tile([P, D], F32, tag="O", name="o_last")
        for c in range(NPASS):
            g = b * NPASS + c
            nc.tensor.matmul_mx(
                out=o_last[:],
                lhsT=eh_codes[c][:].bitcast(FP8X4),
                lhsT_scale=eh_scl[c][:],
                rhs=v_codes[:, g * D:(g + 1) * D].bitcast(FP8X4),
                rhs_scale=v_scl[:, g * D:(g + 1) * D],
                start=(c == 0),
                stop=(c == NPASS - 1),
            )
        stage_out(LAST - 1)
        nc.scalar.activation(out=o_sb[b][:, n, :], in_=o_last[:], func=ACT.Copy, scale=ri_t[:])
        nc.sync.dma_start(out=o_dram[b][:, n:n + 1, :], in_=o_sb[b][:, n:n + 1, :])
